import numpy as np
import ml_dtypes


def mxq(x, axis, fmt="e4m3"):
    dtype, down = {"e4m3": (ml_dtypes.float8_e4m3fn, 7), "e5m2": (ml_dtypes.float8_e5m2, 14)}[fmt]
    v = np.moveaxis(np.asarray(x, np.float32).astype(ml_dtypes.bfloat16).astype(np.float64), axis, -1)
    blocks = v.reshape(v.shape[:-1] + (-1, 32))
    amax = np.abs(blocks).max(-1, keepdims=True)
    byte = np.maximum(np.where(amax > 0, np.frexp(amax)[1] - 1 + 127, 0) - down, 1)
    scale = np.exp2(byte - 127.0)
    codes = (blocks / scale).astype(np.float32).astype(dtype).astype(np.float64)
    return np.moveaxis((codes * scale).reshape(v.shape), -1, axis)


WIDE = False


def mx_kscale(k):
    if not WIDE:
        return np.ones(k)
    levels = np.array([10, -10, 5, -5, 0])
    if k % 512:
        return np.exp2(np.random.permutation(np.resize(levels, k // 32))).repeat(32)
    a = np.empty((k // 512, 16))
    for p in range(k // 512):
        a[p, :8] = np.random.permutation(np.resize(levels, 8))
        for g in range(8):
            far = levels[np.abs(levels - a[p, g]) >= 10]
            a[p, g + 8] = far[np.random.randint(len(far))]
    return np.exp2(a.ravel()).repeat(32)


BF16 = ml_dtypes.bfloat16


def bf(x):
    return np.asarray(x, np.float32).astype(BF16)


def f64(x):
    return np.asarray(x).astype(np.float64)


B, S, D, H, KV, DH, QB = 1, 1024, 1024, 16, 4, 128, 512
HALF = DH // 2
EPS = 1e-6


def rope_tables():
    inv_freq = 1.0 / (10000.0 ** (np.arange(HALF) / HALF))
    ang = np.arange(S)[:, None] * inv_freq[None, :]
    ang = np.concatenate([ang, ang], axis=-1)
    return np.sin(ang), np.cos(ang)


def rmsnorm(u, scale, shift):
    rms = np.sqrt(np.mean(u * u, axis=-1, keepdims=True) + EPS)
    return u / rms * (1.0 + scale) + shift


def apply_rope(u, sin, cos):
    rot = np.concatenate([-u[..., HALF:], u[..., :HALF]], axis=-1)
    return u * cos[None, None, :S, :] + rot * sin[None, None, :S, :]


def heads(u, n):
    return u.reshape(B, S, n, DH).transpose(0, 2, 1, 3)


def setup_inputs():
    s = mx_kscale(D)
    sin, cos = rope_tables()
    return {"x": bf(np.random.standard_normal((B, S, D)) * s),
            "sin_thetas": bf(sin), "cos_thetas": bf(cos),
            "wq": bf(np.random.standard_normal((H * DH, D)) / np.sqrt(D) / s),
            "wk": bf(np.random.standard_normal((KV * DH, D)) / np.sqrt(D) / s),
            "wv": bf(np.random.standard_normal((KV * DH, D)) * 2.0 / np.sqrt(D) / s),
            "q_scale": bf(np.random.standard_normal(DH) * 0.1), "q_shift": bf(np.random.standard_normal(DH) * 0.1),
            "k_scale": bf(np.random.standard_normal(DH) * 0.1), "k_shift": bf(np.random.standard_normal(DH) * 0.1)}


def reference(x, sin_thetas, cos_thetas, wq, wk, wv, q_scale, q_shift, k_scale, k_shift):
    xq = mxq(f64(x), 2, "e4m3")
    q = heads(xq @ mxq(f64(wq), 1, "e4m3").T, H)
    k = heads(xq @ mxq(f64(wk), 1, "e4m3").T, KV)
    v = heads(xq @ mxq(f64(wv), 1, "e4m3").T, KV)
    q = rmsnorm(q, f64(q_scale), f64(q_shift))
    k = rmsnorm(k, f64(k_scale), f64(k_shift))
    q = apply_rope(q, f64(sin_thetas), f64(cos_thetas))
    k = apply_rope(k, f64(sin_thetas), f64(cos_thetas))
    return q, k, v

@@ -1,0 +1,282 @@
+from contextlib import ExitStack
+
+import concourse.mybir as mybir
+from concourse.masks import make_identity
+
+F32 = mybir.dt.float32
+BF16 = mybir.dt.bfloat16
+U32 = mybir.dt.uint32
+U8 = mybir.dt.uint8
+FP8X4 = mybir.dt.float8_e4m3fn_x4
+ALU = mybir.AluOpType
+ACT = mybir.ActivationFunctionType
+
+P = 128
+S = 1024
+D = 1024
+DH = 128
+HALF = DH // 2
+EPS = 1e-6
+TILES = S // P
+PACK = 4
+PASSES = D // (P * PACK)
+CHUNKS = D // 2 // P
+HEADS = 4
+COLS = HEADS * DH
+PAIR = 2
+ROUNDS_PER_GROUP = TILES // PAIR
+BANK_TILES = 512 // DH
+LEAD = 2
+
+FLOPS = 2 * S * D * (16 + 4 + 4) * DH
+
+
+def tile_groupqueryattention_pa_kernel(
+    tc, x, sin_thetas, cos_thetas, wq, wk, wv, q_scale, q_shift, k_scale, k_shift, out_0, out_1, out_2
+):
+    nc = tc.nc
+    with ExitStack() as ctx:
+        keep = ctx.enter_context(tc.tile_pool(name="keep", bufs=1))
+        grouped_pool = ctx.enter_context(tc.tile_pool(name="grouped", bufs=2))
+        weight_pool = ctx.enter_context(tc.tile_pool(name="weights", bufs=2))
+        product_pool = ctx.enter_context(tc.tile_pool(name="products", bufs=3))
+        stage_pool = ctx.enter_context(tc.tile_pool(name="stage", bufs=4))
+        small_pool = ctx.enter_context(tc.tile_pool(name="small", bufs=4))
+        flip_psum = ctx.enter_context(tc.psum_pool(name="flip", bufs=2))
+        offset_psum = ctx.enter_context(tc.psum_pool(name="offset", bufs=2))
+        acc_psum = ctx.enter_context(tc.psum_pool(name="acc", bufs=4))
+        ctx.enter_context(tc.manual_schedule())
+
+        groups = [(wq[COLS * g : COLS * (g + 1), :], out_0[0, HEADS * g : HEADS * (g + 1)], 0) for g in range(4)]
+        groups.append((wk, out_1[0], 1))
+        groups.append((wv, out_2[0], None))
+        rounds = len(groups) * ROUNDS_PER_GROUP
+
+        cos_sb = keep.tile([P, TILES, DH], BF16)
+        sin_sb = keep.tile([P, TILES, DH], BF16)
+        nc.scalar.dma_start(out=cos_sb[:], in_=cos_thetas.rearrange("(p t) d -> p t d", t=TILES))
+        nc.scalar.dma_start(out=sin_sb[:], in_=sin_thetas.rearrange("(p t) d -> p t d", t=TILES))
+        vectors = keep.tile([P, 4, DH], BF16)
+        nc.vector.memset(vectors[:], 0.0)
+        for j, vector in enumerate((q_scale, k_scale, q_shift, k_shift)):
+            nc.scalar.dma_start(out=vectors[0:1, j, :], in_=vector.unsqueeze(0))
+
+        x_sb = keep.tile([P, TILES, D], BF16)
+        x_view = x[0].rearrange("(p t) d -> p t d", t=TILES)
+        w_sb = [keep.tile([P, HEADS, D], BF16, name="w_sb%d" % g) for g in range(len(groups))]
+
+        def load_x(pair):
+            tiles = slice(PAIR * pair, PAIR * (pair + 1))
+            nc.sync.dma_start(out=x_sb[:, tiles, :], in_=x_view[:, tiles, :])
+
+        def load_w(g):
+            nc.sync.dma_start(out=w_sb[g][:], in_=groups[g][0].rearrange("(r p) i -> p r i", p=P))
+
+        load_x(0)
+        load_w(0)
+        for pair in range(1, ROUNDS_PER_GROUP):
+            load_x(pair)
+        for g in range(1, len(groups)):
+            load_w(g)
+
+        ident = keep.tile([P, P], F32)
+        make_identity(nc, ident[:])
+        ones = keep.tile([P, P], BF16)
+        nc.vector.memset(ones[:], 1.0)
+        eps = keep.tile([P, 1], F32)
+        nc.vector.memset(eps[:], EPS)
+
+        spread = flip_psum.tile([P, 4, DH], F32, tag="flip")
+        nc.tensor.matmul(
+            out=spread[:].rearrange("p j d -> p (j d)"),
+            lhsT=ones[:],
+            rhs=vectors[:].rearrange("p j d -> p (j d)"),
+            start=True,
+            stop=True,
+        )
+        low, high = slice(0, HALF), slice(HALF, DH)
+        gain = keep.tile([P, 2, DH], F32)
+        gain_s = keep.tile([P, 2, DH], F32)
+        shift = keep.tile([P, 2, DH], F32)
+        shift_r = keep.tile([P, 2, DH], F32)
+        nc.vector.tensor_scalar_add(out=gain[:], in0=spread[:, 0:2, :], scalar1=1.0)
+        nc.vector.tensor_copy(out=gain_s[:, :, low], in_=gain[:, :, low])
+        nc.vector.tensor_scalar_mul(out=gain_s[:, :, high], in0=gain[:, :, high], scalar1=-1.0)
+        nc.vector.tensor_copy(out=shift[:], in_=spread[:, 2:4, :])
+        nc.vector.tensor_scalar_mul(out=shift_r[:, :, low], in0=spread[:, 2:4, high], scalar1=-1.0)
+        nc.vector.tensor_copy(out=shift_r[:, :, high], in_=spread[:, 2:4, low])
+
+        def over_tiles(vector, width):
+            return vector.unsqueeze(1).to_broadcast([P, TILES, width])
+
+        def make_factors(engine, which):
+            factors = keep.tile([P, TILES, 2, DH], F32, name="factors%d" % which)
+            engine.tensor_tensor(out=factors[:, :, 0, :], in0=cos_sb[:], in1=over_tiles(gain[:, which, :], DH), op=ALU.mult)
+            engine.tensor_tensor(
+                out=factors[:, :, 1, low], in0=sin_sb[:, :, high], in1=over_tiles(gain_s[:, which, low], HALF), op=ALU.mult
+            )
+            engine.tensor_tensor(
+                out=factors[:, :, 1, high], in0=sin_sb[:, :, low], in1=over_tiles(gain_s[:, which, high], HALF), op=ALU.mult
+            )
+            return factors
+
+        offset_sb = keep.tile([P, 2, TILES, DH], F32)
+
+        def make_offset(engine, which):
+            turned = keep.tile([P, TILES, DH], F32, name="turned%d" % which)
+            engine.tensor_tensor(
+                out=offset_sb[:, which], in0=cos_sb[:], in1=over_tiles(shift[:, which, :], DH), op=ALU.mult
+            )
+            engine.tensor_tensor(out=turned[:], in0=sin_sb[:], in1=over_tiles(shift_r[:, which, :], DH), op=ALU.mult)
+            engine.tensor_tensor(out=offset_sb[:, which], in0=offset_sb[:, which], in1=turned[:], op=ALU.add)
+
+        def offsets_into_psum(which, part):
+            offset = offset_psum.tile([P, BANK_TILES, DH], F32)
+            nc.tensor.matmul(
+                out=offset[:].rearrange("p t d -> p (t d)"),
+                lhsT=ident[:],
+                rhs=offset_sb[:, which, BANK_TILES * part : BANK_TILES * (part + 1), :].rearrange("p t d -> p (t d)"),
+                start=True,
+                stop=True,
+            )
+            return offset
+
+        def flip_rows(rows, grouped_words):
+            words = rows.bitcast(F32)
+            flipped = flip_psum.tile([P, CHUNKS, P], F32, tag="flip")
+            for piece in range(CHUNKS):
+                c, u = divmod(piece, 2)
+                nc.tensor.transpose(flipped[:, piece, :], words[:, 2 * P * c + u : 2 * P * (c + 1) : 2], ident[:])
+            nc.scalar.copy(out=grouped_words, in_=flipped[:].rearrange("p (c u) n -> p c n u", u=2))
+
+        x_codes = keep.tile([P, TILES, PASSES, P], U32, align_bytes=64)
+        x_scales = keep.tile([P, TILES, PASSES, P], U8, align_bytes=64)
+
+        def quantise_x(pair):
+            x_grouped = grouped_pool.tile([P, PAIR, PASSES, P, PACK], BF16, align_bytes=64)
+            for i in range(PAIR):
+                flip_rows(x_sb[:, PAIR * pair + i, :], x_grouped[:, i].bitcast(F32))
+            tiles = slice(PAIR * pair, PAIR * (pair + 1))
+            nc.vector.quantize_mx(
+                out=x_codes[:, tiles].rearrange("p t c m -> p (t c m)").bitcast(FP8X4),
+                scales=x_scales[:, tiles].rearrange("p t c m -> p (t c m)"),
+                in_=x_grouped[:].rearrange("p t c m j -> p (t c m j)"),
+            )
+
+        def quantise_w(g):
+            w_grouped = grouped_pool.tile([P, PASSES, COLS, PACK], BF16, align_bytes=64)
+            for r in range(HEADS):
+                flip_rows(w_sb[g][:, r, :], w_grouped[:, :, DH * r : DH * (r + 1), :].bitcast(F32))
+            w_codes = weight_pool.tile([P, PASSES, COLS], U32, align_bytes=64)
+            w_scales = weight_pool.tile([P, PASSES, COLS], U8, align_bytes=64)
+            nc.vector.quantize_mx(
+                out=w_codes[:].rearrange("p c n -> p (c n)").bitcast(FP8X4),
+                scales=w_scales[:].rearrange("p c n -> p (c n)"),
+                in_=w_grouped[:].rearrange("p c n j -> p (c n j)"),
+            )
+            return w_codes, w_scales
+
+        weights = {}
+
+        def prepare(n):
+            g, pair = divmod(n, ROUNDS_PER_GROUP)
+            if g == 0:
+                quantise_x(pair)
+            if pair == 0 and g < len(groups):
+                weights[g] = quantise_w(g)
+
+        def project(t, w_codes, w_scales):
+            acc = acc_psum.tile([P, COLS], F32)
+            for c in range(PASSES):
+                nc.tensor.matmul_mx(
+                    out=acc[:],
+                    lhsT=x_codes[:, t, c, :].bitcast(FP8X4),
+                    lhsT_scale=x_scales[:, t, c, :],
+                    rhs=w_codes[:, c, :].bitcast(FP8X4),
+                    rhs_scale=w_scales[:, c, :],
+                    start=(c == 0),
+                    stop=(c == PASSES - 1),
+                )
+            return acc
+
+        squares = keep.tile([P, DH], F32)
+
+        def rotate(first, w_pair, factors, stage):
+            products = product_pool.tile([P, PAIR, 2, COLS], F32)
+            sum_sq = small_pool.tile([P, PAIR * HEADS], F32)
+            for i in range(PAIR):
+                acc = project(first + i, *w_pair)
+                for h in range(HEADS):
+                    nc.scalar.activation(
+                        out=squares[:],
+                        in_=acc[:, DH * h : DH * (h + 1)],
+                        func=ACT.Square,
+                        accum_out=sum_sq[:, HEADS * i + h : HEADS * i + h + 1],
+                    )
+                nc.vector.tensor_tensor(
+                    out=products[:, i].rearrange("p j (h d) -> p j h d", d=DH),
+                    in0=acc[:].rearrange("p (h d) -> p h d", d=DH).unsqueeze(1).to_broadcast([P, 2, HEADS, DH]),
+                    in1=factors[:, first + i].unsqueeze(2).to_broadcast([P, 2, HEADS, DH]),
+                    op=ALU.mult,
+                )
+            rms = small_pool.tile([P, PAIR * HEADS], F32)
+            nc.scalar.activation(out=rms[:], in_=sum_sq[:], func=ACT.Sqrt, scale=1.0 / DH, bias=eps[:, 0:1])
+            r = small_pool.tile([P, PAIR * HEADS], F32)
+            nc.vector.reciprocal(out=r[:], in_=rms[:])
+            straight = products[:, :, 0, :].rearrange("p i (h d) -> p i h d", d=DH)
+            crossed = products[:, :, 1, :].rearrange("p i (h d) -> p i h d", d=DH)
+            rotated = stage[:].rearrange("p h i d -> p i h d")
+            nc.gpsimd.tensor_tensor(
+                out=rotated[:, :, :, low], in0=straight[:, :, :, low], in1=crossed[:, :, :, high], op=ALU.add
+            )
+            nc.gpsimd.tensor_tensor(
+                out=rotated[:, :, :, high], in0=straight[:, :, :, high], in1=crossed[:, :, :, low], op=ALU.add
+            )
+            return r
+
+        offsets = {}
+
+        def finish(first, stage, r, which, out_rows):
+            part = first // BANK_TILES
+            if (which, part) not in offsets:
+                offsets[(which, part)] = offsets_into_psum(which, part)
+            offset = offsets[(which, part)]
+            for i in range(PAIR):
+                for h in range(HEADS):
+                    nc.vector.scalar_tensor_tensor(
+                        out=stage[:, h, i, :],
+                        in0=stage[:, h, i, :],
+                        scalar=r[:, HEADS * i + h : HEADS * i + h + 1],
+                        in1=offset[:, first + i - BANK_TILES * part, :],
+                        op0=ALU.mult,
+                        op1=ALU.add,
+                    )
+            nc.sync.dma_start(out=out_rows, in_=stage[:])
+
+        factors = [make_factors(nc.vector, 0), make_factors(nc.vector, 1)]
+        make_offset(nc.gpsimd, 0)
+        quantise_x(0)
+        make_offset(nc.vector, 1)
+        weights[0] = quantise_w(0)
+        quantise_x(1)
+
+        waiting = None
+        for n in range(rounds):
+            g, pair = divmod(n, ROUNDS_PER_GROUP)
+            first = PAIR * pair
+            which = groups[g][2]
+            out_rows = groups[g][1].rearrange("h (p t) d -> p h t d", t=TILES)[:, :, first : first + PAIR, :]
+            stage = stage_pool.tile([P, HEADS, PAIR, DH], F32)
+            if which is None:
+                for i in range(PAIR):
+                    acc = project(first + i, *weights[g])
+                    nc.scalar.copy(out=stage[:, :, i, :], in_=acc[:].rearrange("p (h d) -> p h d", d=DH))
+                nc.sync.dma_start(out=out_rows, in_=stage[:])
+                begun = None
+            else:
+                r = rotate(first, weights[g], factors[which], stage)
+                begun = (first, stage, r, which, out_rows)
+            prepare(n + LEAD)
+            if waiting is not None:
+                finish(*waiting)
+            waiting = begun

@@ -24,9 +24,9 @@ CHUNKS = D // 2 // P
 HEADS = 4
 COLS = HEADS * DH
 PAIR = 2
-ROUNDS_PER_GROUP = TILES // PAIR
+PAIRS = TILES // PAIR
 BANK_TILES = 512 // DH
-LEAD = 2
+LAG = 1
 
 FLOPS = 2 * S * D * (16 + 4 + 4) * DH
 
@@ -38,10 +38,9 @@ def tile_groupqueryattention_pa_kernel(
     with ExitStack() as ctx:
         keep = ctx.enter_context(tc.tile_pool(name="keep", bufs=1))
         grouped_pool = ctx.enter_context(tc.tile_pool(name="grouped", bufs=2))
-        weight_pool = ctx.enter_context(tc.tile_pool(name="weights", bufs=2))
-        product_pool = ctx.enter_context(tc.tile_pool(name="products", bufs=3))
-        stage_pool = ctx.enter_context(tc.tile_pool(name="stage", bufs=4))
-        small_pool = ctx.enter_context(tc.tile_pool(name="small", bufs=4))
+        product_pool = ctx.enter_context(tc.tile_pool(name="products", bufs=LAG + 2))
+        stage_pool = ctx.enter_context(tc.tile_pool(name="stage", bufs=LAG + 3))
+        small_pool = ctx.enter_context(tc.tile_pool(name="small", bufs=LAG + 3))
         flip_psum = ctx.enter_context(tc.psum_pool(name="flip", bufs=2))
         offset_psum = ctx.enter_context(tc.psum_pool(name="offset", bufs=2))
         acc_psum = ctx.enter_context(tc.psum_pool(name="acc", bufs=4))
@@ -49,13 +48,9 @@ def tile_groupqueryattention_pa_kernel(
 
         groups = [(wq[COLS * g : COLS * (g + 1), :], out_0[0, HEADS * g : HEADS * (g + 1)], 0) for g in range(4)]
         groups.append((wk, out_1[0], 1))
+        VALUES = len(groups)
         groups.append((wv, out_2[0], None))
-        rounds = len(groups) * ROUNDS_PER_GROUP
 
-        cos_sb = keep.tile([P, TILES, DH], BF16)
-        sin_sb = keep.tile([P, TILES, DH], BF16)
-        nc.scalar.dma_start(out=cos_sb[:], in_=cos_thetas.rearrange("(p t) d -> p t d", t=TILES))
-        nc.scalar.dma_start(out=sin_sb[:], in_=sin_thetas.rearrange("(p t) d -> p t d", t=TILES))
         vectors = keep.tile([P, 4, DH], BF16)
         nc.vector.memset(vectors[:], 0.0)
         for j, vector in enumerate((q_scale, k_scale, q_shift, k_shift)):
@@ -64,136 +59,168 @@ def tile_groupqueryattention_pa_kernel(
         x_sb = keep.tile([P, TILES, D], BF16)
         x_view = x[0].rearrange("(p t) d -> p t d", t=TILES)
         w_sb = [keep.tile([P, HEADS, D], BF16, name="w_sb%d" % g) for g in range(len(groups))]
+        cos_sb = keep.tile([P, TILES, DH], BF16)
+        sin_sb = keep.tile([P, TILES, DH], BF16)
 
         def load_x(pair):
             tiles = slice(PAIR * pair, PAIR * (pair + 1))
             nc.sync.dma_start(out=x_sb[:, tiles, :], in_=x_view[:, tiles, :])
 
-        def load_w(g):
-            nc.sync.dma_start(out=w_sb[g][:], in_=groups[g][0].rearrange("(r p) i -> p r i", p=P))
+        def load_w(g, rows=slice(0, HEADS)):
+            nc.sync.dma_start(out=w_sb[g][:, rows, :], in_=groups[g][0].rearrange("(r p) i -> p r i", p=P)[:, rows, :])
 
         load_x(0)
-        load_w(0)
-        for pair in range(1, ROUNDS_PER_GROUP):
+        load_w(0, slice(0, 2))
+        load_w(0, slice(2, 4))
+        nc.sync.dma_start(out=cos_sb[:], in_=cos_thetas.rearrange("(p t) d -> p t d", t=TILES))
+        nc.sync.dma_start(out=sin_sb[:], in_=sin_thetas.rearrange("(p t) d -> p t d", t=TILES))
+        for pair in range(1, PAIRS):
             load_x(pair)
-        for g in range(1, len(groups)):
+        for g in (1, 2, VALUES, 3, 4):
             load_w(g)
 
-        ident = keep.tile([P, P], F32)
-        make_identity(nc, ident[:])
-        ones = keep.tile([P, P], BF16)
-        nc.vector.memset(ones[:], 1.0)
         eps = keep.tile([P, 1], F32)
         nc.vector.memset(eps[:], EPS)
+        ones = keep.tile([P, P], BF16)
+        nc.vector.memset(ones[:], 1.0)
+        first_root = keep.tile([P, 1], F32)
+        nc.scalar.activation(out=first_root[:], in_=eps[:], func=ACT.Sqrt)
+        ident = keep.tile([P, P], F32)
+        make_identity(nc, ident[:])
+        ident_b = keep.tile([P, P], BF16)
+        nc.vector.tensor_copy(out=ident_b[:], in_=ident[:])
 
-        spread = flip_psum.tile([P, 4, DH], F32, tag="flip")
-        nc.tensor.matmul(
-            out=spread[:].rearrange("p j d -> p (j d)"),
-            lhsT=ones[:],
-            rhs=vectors[:].rearrange("p j d -> p (j d)"),
-            start=True,
-            stop=True,
-        )
-        low, high = slice(0, HALF), slice(HALF, DH)
-        gain = keep.tile([P, 2, DH], F32)
-        gain_s = keep.tile([P, 2, DH], F32)
-        shift = keep.tile([P, 2, DH], F32)
-        shift_r = keep.tile([P, 2, DH], F32)
-        nc.vector.tensor_scalar_add(out=gain[:], in0=spread[:, 0:2, :], scalar1=1.0)
-        nc.vector.tensor_copy(out=gain_s[:, :, low], in_=gain[:, :, low])
-        nc.vector.tensor_scalar_mul(out=gain_s[:, :, high], in0=gain[:, :, high], scalar1=-1.0)
-        nc.vector.tensor_copy(out=shift[:], in_=spread[:, 2:4, :])
-        nc.vector.tensor_scalar_mul(out=shift_r[:, :, low], in0=spread[:, 2:4, high], scalar1=-1.0)
-        nc.vector.tensor_copy(out=shift_r[:, :, high], in_=spread[:, 2:4, low])
-
-        def over_tiles(vector, width):
-            return vector.unsqueeze(1).to_broadcast([P, TILES, width])
-
-        def make_factors(engine, which):
-            factors = keep.tile([P, TILES, 2, DH], F32, name="factors%d" % which)
-            engine.tensor_tensor(out=factors[:, :, 0, :], in0=cos_sb[:], in1=over_tiles(gain[:, which, :], DH), op=ALU.mult)
-            engine.tensor_tensor(
-                out=factors[:, :, 1, low], in0=sin_sb[:, :, high], in1=over_tiles(gain_s[:, which, low], HALF), op=ALU.mult
-            )
-            engine.tensor_tensor(
-                out=factors[:, :, 1, high], in0=sin_sb[:, :, low], in1=over_tiles(gain_s[:, which, high], HALF), op=ALU.mult
-            )
-            return factors
-
-        offset_sb = keep.tile([P, 2, TILES, DH], F32)
-
-        def make_offset(engine, which):
-            turned = keep.tile([P, TILES, DH], F32, name="turned%d" % which)
-            engine.tensor_tensor(
-                out=offset_sb[:, which], in0=cos_sb[:], in1=over_tiles(shift[:, which, :], DH), op=ALU.mult
-            )
-            engine.tensor_tensor(out=turned[:], in0=sin_sb[:], in1=over_tiles(shift_r[:, which, :], DH), op=ALU.mult)
-            engine.tensor_tensor(out=offset_sb[:, which], in0=offset_sb[:, which], in1=turned[:], op=ALU.add)
-
-        def offsets_into_psum(which, part):
-            offset = offset_psum.tile([P, BANK_TILES, DH], F32)
-            nc.tensor.matmul(
-                out=offset[:].rearrange("p t d -> p (t d)"),
-                lhsT=ident[:],
-                rhs=offset_sb[:, which, BANK_TILES * part : BANK_TILES * (part + 1), :].rearrange("p t d -> p (t d)"),
-                start=True,
-                stop=True,
-            )
-            return offset
-
-        def flip_rows(rows, grouped_words):
+        def flip_rows(rows, grouped_words, copy, bank):
             words = rows.bitcast(F32)
-            flipped = flip_psum.tile([P, CHUNKS, P], F32, tag="flip")
+            flipped = bank()
             for piece in range(CHUNKS):
                 c, u = divmod(piece, 2)
                 nc.tensor.transpose(flipped[:, piece, :], words[:, 2 * P * c + u : 2 * P * (c + 1) : 2], ident[:])
-            nc.scalar.copy(out=grouped_words, in_=flipped[:].rearrange("p (c u) n -> p c n u", u=2))
+            copy(out=grouped_words, in_=flipped[:].rearrange("p (c u) n -> p c n u", u=2))
+
+        def flip_bank():
+            return flip_psum.tile([P, CHUNKS, P], F32, name="flipped", tag="flip")
+
+        def acc_bank():
+            return acc_psum.tile([P, CHUNKS, P], F32, name="flipped_early", tag="acc")
 
         x_codes = keep.tile([P, TILES, PASSES, P], U32, align_bytes=64)
         x_scales = keep.tile([P, TILES, PASSES, P], U8, align_bytes=64)
+        w_codes = [keep.tile([P, PASSES, COLS], U32, align_bytes=64, name="w_codes%d" % g) for g in range(len(groups))]
+        w_scales = [keep.tile([P, PASSES, COLS], U8, align_bytes=64, name="w_scales%d" % g) for g in range(len(groups))]
+        grouped = {}
+
+        def flip_x(pair, i, copy=nc.scalar.copy, bank=flip_bank):
+            if ("x", pair) not in grouped:
+                grouped[("x", pair)] = grouped_pool.tile([P, PAIR, PASSES, P, PACK], BF16, align_bytes=64, name="x_grouped")
+            flip_rows(x_sb[:, PAIR * pair + i, :], grouped[("x", pair)][:, i].bitcast(F32), copy, bank)
+
+        def flip_w(g, r, copy=nc.scalar.copy, bank=flip_bank):
+            if ("w", g) not in grouped:
+                grouped[("w", g)] = grouped_pool.tile([P, PASSES, COLS, PACK], BF16, align_bytes=64, name="w_grouped")
+            flip_rows(w_sb[g][:, r, :], grouped[("w", g)][:, :, DH * r : DH * (r + 1), :].bitcast(F32), copy, bank)
 
         def quantise_x(pair):
-            x_grouped = grouped_pool.tile([P, PAIR, PASSES, P, PACK], BF16, align_bytes=64)
-            for i in range(PAIR):
-                flip_rows(x_sb[:, PAIR * pair + i, :], x_grouped[:, i].bitcast(F32))
             tiles = slice(PAIR * pair, PAIR * (pair + 1))
             nc.vector.quantize_mx(
                 out=x_codes[:, tiles].rearrange("p t c m -> p (t c m)").bitcast(FP8X4),
                 scales=x_scales[:, tiles].rearrange("p t c m -> p (t c m)"),
-                in_=x_grouped[:].rearrange("p t c m j -> p (t c m j)"),
+                in_=grouped[("x", pair)][:].rearrange("p t c m j -> p (t c m j)"),
             )
 
         def quantise_w(g):
-            w_grouped = grouped_pool.tile([P, PASSES, COLS, PACK], BF16, align_bytes=64)
-            for r in range(HEADS):
-                flip_rows(w_sb[g][:, r, :], w_grouped[:, :, DH * r : DH * (r + 1), :].bitcast(F32))
-            w_codes = weight_pool.tile([P, PASSES, COLS], U32, align_bytes=64)
-            w_scales = weight_pool.tile([P, PASSES, COLS], U8, align_bytes=64)
             nc.vector.quantize_mx(
-                out=w_codes[:].rearrange("p c n -> p (c n)").bitcast(FP8X4),
-                scales=w_scales[:].rearrange("p c n -> p (c n)"),
-                in_=w_grouped[:].rearrange("p c n j -> p (c n j)"),
+                out=w_codes[g][:].rearrange("p c n -> p (c n)").bitcast(FP8X4),
+                scales=w_scales[g][:].rearrange("p c n -> p (c n)"),
+                in_=grouped[("w", g)][:].rearrange("p c n j -> p (c n j)"),
             )
-            return w_codes, w_scales
 
-        weights = {}
+        low, high = slice(0, HALF), slice(HALF, DH)
+        straight = keep.tile([P, 2, DH], BF16)
+        swapped = keep.tile([P, 2, DH], BF16)
+        for which in range(2):
+            nc.gpsimd.tensor_copy(out=straight[:, which, :], in_=ident[:])
+            nc.gpsimd.tensor_copy(out=swapped[:, which, low], in_=ident[:, high])
+            nc.gpsimd.tensor_scalar(
+                out=swapped[:, which, high], in0=ident[:, low], scalar1=-1.0, scalar2=0.0, op0=ALU.mult, op1=ALU.add
+            )
+        scaled = keep.tile([P, 2, DH], BF16)
+        scaled_swapped = keep.tile([P, 2, DH], BF16)
+        shifted = keep.tile([P, 2, DH], BF16)
+        shifted_turned = keep.tile([P, 2, DH], BF16)
 
-        def prepare(n):
-            g, pair = divmod(n, ROUNDS_PER_GROUP)
-            if g == 0:
-                quantise_x(pair)
-            if pair == 0 and g < len(groups):
-                weights[g] = quantise_w(g)
+        def make_matrices():
+            spread = offset_psum.tile([P, 4, DH], F32, name="spread", tag="offset")
+            nc.tensor.matmul(
+                out=spread[:].rearrange("p j d -> p (j d)"),
+                lhsT=ones[:],
+                rhs=vectors[:].rearrange("p j d -> p (j d)"),
+                start=True,
+                stop=True,
+            )
+            scale, shift = spread[:, 0:2, :], spread[:, 2:4, :]
+            nc.vector.tensor_tensor(out=scaled[:], in0=scale, in1=straight[:], op=ALU.mult)
+            nc.vector.tensor_tensor(out=scaled_swapped[:], in0=scale, in1=swapped[:], op=ALU.mult)
+            nc.vector.tensor_tensor(out=shifted[:], in0=shift, in1=straight[:], op=ALU.mult)
+            nc.vector.scalar_tensor_tensor(
+                out=shifted_turned[:, :, low],
+                in0=shift[:, :, high],
+                scalar=-1.0,
+                in1=straight[:, :, low],
+                op0=ALU.mult,
+                op1=ALU.mult,
+            )
+            nc.vector.tensor_tensor(
+                out=shifted_turned[:, :, high], in0=shift[:, :, low], in1=straight[:, :, high], op=ALU.mult
+            )
 
-        def project(t, w_codes, w_scales):
-            acc = acc_psum.tile([P, COLS], F32)
+        turned = keep.tile([P, 2, TILES, P], BF16)
+        factors = keep.tile([P, TILES, 2, 2, DH], F32)
+
+        def turn_angles(pair):
+            flipped = flip_psum.tile([P, 2, PAIR, P], BF16, name="angles", tag="flip")
+            for j, table in enumerate((cos_sb, sin_sb)):
+                for i in range(PAIR):
+                    nc.tensor.transpose(flipped[:, j, i, :], table[:, PAIR * pair + i, :], ident_b[:])
+            nc.scalar.copy(out=turned[:, :, PAIR * pair : PAIR * (pair + 1), :], in_=flipped[:])
+
+        def make_factors(pair):
+            for t in range(PAIR * pair, PAIR * (pair + 1)):
+                table = flip_psum.tile([P, 2, 2, DH], F32, name="table", tag="flip")
+                for j, terms in enumerate(((straight, scaled), (swapped, scaled_swapped))):
+                    for k, term in enumerate(terms):
+                        nc.tensor.matmul(
+                            out=table[:, j].rearrange("p w d -> p (w d)"),
+                            lhsT=turned[:, j, t, :],
+                            rhs=term[:].rearrange("p w d -> p (w d)"),
+                            start=(k == 0),
+                            stop=(k == 1),
+                        )
+                nc.scalar.copy(out=factors[:, t], in_=table[:])
+
+        offsets = {}
+
+        def make_offset(which, part):
+            offset = offset_psum.tile([P, BANK_TILES, DH], F32, tag="offset")
+            for i in range(BANK_TILES):
+                for j, term in enumerate((shifted, shifted_turned)):
+                    nc.tensor.matmul(
+                        out=offset[:, i, :],
+                        lhsT=turned[:, j, BANK_TILES * part + i, :],
+                        rhs=term[:, which, :],
+                        start=(j == 0),
+                        stop=(j == 1),
+                    )
+            offsets[(which, part)] = offset
+
+        def project(t, g, acc):
             for c in range(PASSES):
                 nc.tensor.matmul_mx(
                     out=acc[:],
                     lhsT=x_codes[:, t, c, :].bitcast(FP8X4),
                     lhsT_scale=x_scales[:, t, c, :],
-                    rhs=w_codes[:, c, :].bitcast(FP8X4),
-                    rhs_scale=w_scales[:, c, :],
+                    rhs=w_codes[g][:, c, :].bitcast(FP8X4),
+                    rhs_scale=w_scales[g][:, c, :],
                     start=(c == 0),
                     stop=(c == PASSES - 1),
                 )
@@ -201,82 +228,118 @@ def tile_groupqueryattention_pa_kernel(
 
         squares = keep.tile([P, DH], F32)
 
-        def rotate(first, w_pair, factors, stage):
-            products = product_pool.tile([P, PAIR, 2, COLS], F32)
-            sum_sq = small_pool.tile([P, PAIR * HEADS], F32)
-            for i in range(PAIR):
-                acc = project(first + i, *w_pair)
-                for h in range(HEADS):
-                    nc.scalar.activation(
-                        out=squares[:],
-                        in_=acc[:, DH * h : DH * (h + 1)],
-                        func=ACT.Square,
-                        accum_out=sum_sq[:, HEADS * i + h : HEADS * i + h + 1],
-                    )
-                nc.vector.tensor_tensor(
-                    out=products[:, i].rearrange("p j (h d) -> p j h d", d=DH),
-                    in0=acc[:].rearrange("p (h d) -> p h d", d=DH).unsqueeze(1).to_broadcast([P, 2, HEADS, DH]),
-                    in1=factors[:, first + i].unsqueeze(2).to_broadcast([P, 2, HEADS, DH]),
-                    op=ALU.mult,
+        def multiply(acc, t, g, products, i, sum_sq):
+            nc.vector.tensor_tensor(
+                out=products[:, i].rearrange("p j (h d) -> p j h d", d=DH),
+                in0=acc[:].rearrange("p (h d) -> p h d", d=DH).unsqueeze(1).to_broadcast([P, 2, HEADS, DH]),
+                in1=factors[:, t, :, groups[g][2], :].unsqueeze(2).to_broadcast([P, 2, HEADS, DH]),
+                op=ALU.mult,
+            )
+            for h in range(HEADS):
+                nc.scalar.activation(
+                    out=squares[:],
+                    in_=acc[:, DH * h : DH * (h + 1)],
+                    func=ACT.Square,
+                    accum_out=sum_sq[:, HEADS * i + h : HEADS * i + h + 1],
                 )
-            rms = small_pool.tile([P, PAIR * HEADS], F32)
-            nc.scalar.activation(out=rms[:], in_=sum_sq[:], func=ACT.Sqrt, scale=1.0 / DH, bias=eps[:, 0:1])
-            r = small_pool.tile([P, PAIR * HEADS], F32)
-            nc.vector.reciprocal(out=r[:], in_=rms[:])
+
+        def out_rows(g, pair):
+            rows = groups[g][1].rearrange("h (p t) d -> p h t d", t=TILES)
+            return rows[:, :, PAIR * pair : PAIR * (pair + 1), :]
+
+        def add_halves(products, stage):
             straight = products[:, :, 0, :].rearrange("p i (h d) -> p i h d", d=DH)
             crossed = products[:, :, 1, :].rearrange("p i (h d) -> p i h d", d=DH)
             rotated = stage[:].rearrange("p h i d -> p i h d")
-            nc.gpsimd.tensor_tensor(
-                out=rotated[:, :, :, low], in0=straight[:, :, :, low], in1=crossed[:, :, :, high], op=ALU.add
-            )
-            nc.gpsimd.tensor_tensor(
-                out=rotated[:, :, :, high], in0=straight[:, :, :, high], in1=crossed[:, :, :, low], op=ALU.add
-            )
-            return r
+            for here, there in ((low, high), (high, low)):
+                nc.gpsimd.tensor_tensor(
+                    out=rotated[:, :, :, here], in0=straight[:, :, :, here], in1=crossed[:, :, :, there], op=ALU.add
+                )
 
-        offsets = {}
-
-        def finish(first, stage, r, which, out_rows):
-            part = first // BANK_TILES
-            if (which, part) not in offsets:
-                offsets[(which, part)] = offsets_into_psum(which, part)
+        def finish(g, pair, stage, rms):
+            which, part = groups[g][2], PAIR * pair // BANK_TILES
             offset = offsets[(which, part)]
             for i in range(PAIR):
                 for h in range(HEADS):
                     nc.vector.scalar_tensor_tensor(
                         out=stage[:, h, i, :],
                         in0=stage[:, h, i, :],
-                        scalar=r[:, HEADS * i + h : HEADS * i + h + 1],
-                        in1=offset[:, first + i - BANK_TILES * part, :],
+                        scalar=rms[:, HEADS * i + h : HEADS * i + h + 1],
+                        in1=offset[:, PAIR * pair + i - BANK_TILES * part, :],
                         op0=ALU.mult,
                         op1=ALU.add,
                     )
-            nc.sync.dma_start(out=out_rows, in_=stage[:])
+            nc.sync.dma_start(out=out_rows(g, pair), in_=stage[:])
 
-        factors = [make_factors(nc.vector, 0), make_factors(nc.vector, 1)]
-        make_offset(nc.gpsimd, 0)
+        def values(pair):
+            stage = stage_pool.tile([P, HEADS, PAIR, DH], F32, name="stage_v")
+            for i in range(PAIR):
+                acc = project(PAIR * pair + i, VALUES, flip_psum.tile([P, COLS], F32, name="acc_v", tag="flip"))
+                nc.scalar.copy(out=stage[:, :, i, :], in_=acc[:].rearrange("p (h d) -> p h d", d=DH))
+            nc.sync.dma_start(out=out_rows(VALUES, pair), in_=stage[:])
+
+        flip_x(0, 0)
+        flip_x(0, 1, nc.vector.tensor_copy)
+        flip_w(0, 0, nc.scalar.copy, acc_bank)
+        flip_w(0, 1, nc.vector.tensor_copy, acc_bank)
         quantise_x(0)
-        make_offset(nc.vector, 1)
-        weights[0] = quantise_w(0)
-        quantise_x(1)
+        flip_w(0, 2, nc.scalar.copy, acc_bank)
+        flip_w(0, 3, nc.vector.tensor_copy, acc_bank)
+        make_matrices()
+        turn_angles(0)
+        quantise_w(0)
+        make_factors(0)
 
-        waiting = None
-        for n in range(rounds):
-            g, pair = divmod(n, ROUNDS_PER_GROUP)
-            first = PAIR * pair
-            which = groups[g][2]
-            out_rows = groups[g][1].rearrange("h (p t) d -> p h t d", t=TILES)[:, :, first : first + PAIR, :]
+        flips = {
+            0: [("x", 2, 0), ("x", 2, 1), ("w", 1, 0)],
+            1: [("x", 3, 0), ("x", 3, 1), ("w", 1, 1)],
+            2: [("w", 1, 2), ("w", 1, 3)],
+        }
+        for n, g in ((4, 2), (6, VALUES), (8, 3), (12, 4)):
+            flips[n] = [("w", g, 0), ("w", g, 1)]
+            flips[n + 1] = [("w", g, 2), ("w", g, 3)]
+        quantise = {0: ("x", 1), 1: ("x", 2), 2: ("x", 3), 3: ("w", 1), 6: ("w", 2), 8: ("w", VALUES), 10: ("w", 3), 14: ("w", 4)}
+        offset_in = {0: (0, 0), 2: (0, 1), 16: (1, 0), 17: (1, 1)}
+        values_in = {10: 0, 11: 1, 14: 2, 15: 3}
+        rounds = [(g, pair) for g in range(VALUES) for pair in range(PAIRS)]
+
+        def project_round(n):
+            g, pair = rounds[n]
+            return [project(PAIR * pair + i, g, acc_psum.tile([P, COLS], F32, name="acc", tag="acc")) for i in range(PAIR)]
+
+        accs = project_round(0)
+        flip_x(1, 0)
+        flip_x(1, 1)
+        begun = []
+        rms = None
+        for n, (g, pair) in enumerate(rounds):
+            products = product_pool.tile([P, PAIR, 2, COLS], F32)
+            sum_sq = small_pool.tile([P, PAIR * HEADS], F32)
             stage = stage_pool.tile([P, HEADS, PAIR, DH], F32)
-            if which is None:
-                for i in range(PAIR):
-                    acc = project(first + i, *weights[g])
-                    nc.scalar.copy(out=stage[:, :, i, :], in_=acc[:].rearrange("p (h d) -> p h d", d=DH))
-                nc.sync.dma_start(out=out_rows, in_=stage[:])
-                begun = None
-            else:
-                r = rotate(first, weights[g], factors[which], stage)
-                begun = (first, stage, r, which, out_rows)
-            prepare(n + LEAD)
-            if waiting is not None:
-                finish(*waiting)
-            waiting = begun
+            multiply(accs[0], PAIR * pair, g, products, 0, sum_sq)
+            if n > 0:
+                nc.vector.reciprocal(out=rms[:], in_=rms[:])
+            if n in quantise:
+                kind, which = quantise[n]
+                (quantise_x if kind == "x" else quantise_w)(which)
+            multiply(accs[1], PAIR * pair + 1, g, products, 1, sum_sq)
+            if n + 1 < len(rounds):
+                accs = project_round(n + 1)
+            add_halves(products, stage)
+            rms = small_pool.tile([P, PAIR * HEADS], F32)
+            nc.scalar.activation(out=rms[:], in_=sum_sq[:], func=ACT.Sqrt, scale=1.0 / DH, bias=eps[:, 0:1])
+            if n + 1 < PAIRS:
+                turn_angles(n + 1)
+                make_factors(n + 1)
+            if n in offset_in:
+                make_offset(*offset_in[n])
+            for kind, which, i in flips.get(n, []):
+                (flip_x if kind == "x" else flip_w)(which, i)
+            if n in values_in:
+                values(values_in[n])
+            begun.append((g, pair, stage, rms))
+            if n >= LAG:
+                finish(*begun[n - LAG])
+        nc.vector.reciprocal(out=rms[:], in_=rms[:])
+        for n in range(len(rounds) - LAG, len(rounds)):
+            finish(*begun[n])

@@ -40,6 +40,7 @@ def tile_groupqueryattention_pa_kernel(
         grouped_pool = ctx.enter_context(tc.tile_pool(name="grouped", bufs=2))
         product_pool = ctx.enter_context(tc.tile_pool(name="products", bufs=LAG + 2))
         stage_pool = ctx.enter_context(tc.tile_pool(name="stage", bufs=LAG + 3))
+        square_pool = ctx.enter_context(tc.tile_pool(name="squares", bufs=2))
         small_pool = ctx.enter_context(tc.tile_pool(name="small", bufs=LAG + 3))
         flip_psum = ctx.enter_context(tc.psum_pool(name="flip", bufs=2))
         offset_psum = ctx.enter_context(tc.psum_pool(name="offset", bufs=2))
@@ -226,9 +227,8 @@ def tile_groupqueryattention_pa_kernel(
                 )
             return acc
 
-        squares = keep.tile([P, DH], F32)
 
-        def multiply(acc, t, g, products, i, sum_sq):
+        def multiply(acc, t, g, products, i, squares, sum_sq):
             nc.vector.tensor_tensor(
                 out=products[:, i].rearrange("p j (h d) -> p j h d", d=DH),
                 in0=acc[:].rearrange("p (h d) -> p h d", d=DH).unsqueeze(1).to_broadcast([P, 2, HEADS, DH]),
@@ -237,7 +237,7 @@ def tile_groupqueryattention_pa_kernel(
             )
             for h in range(HEADS):
                 nc.scalar.activation(
-                    out=squares[:],
+                    out=squares[:, HEADS * i + h, :],
                     in_=acc[:, DH * h : DH * (h + 1)],
                     func=ACT.Square,
                     accum_out=sum_sq[:, HEADS * i + h : HEADS * i + h + 1],
@@ -315,14 +315,15 @@ def tile_groupqueryattention_pa_kernel(
         for n, (g, pair) in enumerate(rounds):
             products = product_pool.tile([P, PAIR, 2, COLS], F32)
             sum_sq = small_pool.tile([P, PAIR * HEADS], F32)
+            squares = square_pool.tile([P, PAIR * HEADS, DH], F32)
             stage = stage_pool.tile([P, HEADS, PAIR, DH], F32)
-            multiply(accs[0], PAIR * pair, g, products, 0, sum_sq)
+            multiply(accs[0], PAIR * pair, g, products, 0, squares, sum_sq)
             if n > 0:
                 nc.vector.reciprocal(out=rms[:], in_=rms[:])
             if n in quantise:
                 kind, which = quantise[n]
                 (quantise_x if kind == "x" else quantise_w)(which)
-            multiply(accs[1], PAIR * pair + 1, g, products, 1, sum_sq)
+            multiply(accs[1], PAIR * pair + 1, g, products, 1, squares, sum_sq)
             if n + 1 < len(rounds):
                 accs = project_round(n + 1)
             add_halves(products, stage)

@@ -26,7 +26,7 @@ COLS = HEADS * DH
 PAIR = 2
 PAIRS = TILES // PAIR
 BANK_TILES = 512 // DH
-LAG = 1
+LAG = 2
 
 FLOPS = 2 * S * D * (16 + 4 + 4) * DH
 
@@ -38,8 +38,9 @@ def tile_groupqueryattention_pa_kernel(
     with ExitStack() as ctx:
         keep = ctx.enter_context(tc.tile_pool(name="keep", bufs=1))
         grouped_pool = ctx.enter_context(tc.tile_pool(name="grouped", bufs=2))
-        product_pool = ctx.enter_context(tc.tile_pool(name="products", bufs=LAG + 2))
+        product_pool = ctx.enter_context(tc.tile_pool(name="products", bufs=3))
         stage_pool = ctx.enter_context(tc.tile_pool(name="stage", bufs=LAG + 3))
+        value_pool = ctx.enter_context(tc.tile_pool(name="values", bufs=2))
         square_pool = ctx.enter_context(tc.tile_pool(name="squares", bufs=2))
         small_pool = ctx.enter_context(tc.tile_pool(name="small", bufs=LAG + 3))
         flip_psum = ctx.enter_context(tc.psum_pool(name="flip", bufs=2))
@@ -85,19 +86,19 @@ def tile_groupqueryattention_pa_kernel(
         ones = keep.tile([P, P], BF16)
         nc.vector.memset(ones[:], 1.0)
         first_root = keep.tile([P, 1], F32)
-        nc.scalar.activation(out=first_root[:], in_=eps[:], func=ACT.Sqrt)
+        nc.scalar.activation(out=first_root[:], in_=eps[:], func=ACT.Abs_reciprocal_sqrt)
         ident = keep.tile([P, P], F32)
         make_identity(nc, ident[:])
         ident_b = keep.tile([P, P], BF16)
         nc.vector.tensor_copy(out=ident_b[:], in_=ident[:])
 
-        def flip_rows(rows, grouped_words, copy, bank):
+        def flip_rows(rows, grouped_words, bank):
             words = rows.bitcast(F32)
             flipped = bank()
             for piece in range(CHUNKS):
                 c, u = divmod(piece, 2)
                 nc.tensor.transpose(flipped[:, piece, :], words[:, 2 * P * c + u : 2 * P * (c + 1) : 2], ident[:])
-            copy(out=grouped_words, in_=flipped[:].rearrange("p (c u) n -> p c n u", u=2))
+            return grouped_words, flipped[:].rearrange("p (c u) n -> p c n u", u=2)
 
         def flip_bank():
             return flip_psum.tile([P, CHUNKS, P], F32, name="flipped", tag="flip")
@@ -111,15 +112,19 @@ def tile_groupqueryattention_pa_kernel(
         w_scales = [keep.tile([P, PASSES, COLS], U8, align_bytes=64, name="w_scales%d" % g) for g in range(len(groups))]
         grouped = {}
 
-        def flip_x(pair, i, copy=nc.scalar.copy, bank=flip_bank):
+        def flip_x(pair, i, bank=flip_bank):
             if ("x", pair) not in grouped:
                 grouped[("x", pair)] = grouped_pool.tile([P, PAIR, PASSES, P, PACK], BF16, align_bytes=64, name="x_grouped")
-            flip_rows(x_sb[:, PAIR * pair + i, :], grouped[("x", pair)][:, i].bitcast(F32), copy, bank)
+            return flip_rows(x_sb[:, PAIR * pair + i, :], grouped[("x", pair)][:, i].bitcast(F32), bank)
 
-        def flip_w(g, r, copy=nc.scalar.copy, bank=flip_bank):
+        def flip_w(g, r, bank=flip_bank):
             if ("w", g) not in grouped:
                 grouped[("w", g)] = grouped_pool.tile([P, PASSES, COLS, PACK], BF16, align_bytes=64, name="w_grouped")
-            flip_rows(w_sb[g][:, r, :], grouped[("w", g)][:, :, DH * r : DH * (r + 1), :].bitcast(F32), copy, bank)
+            return flip_rows(w_sb[g][:, r, :], grouped[("w", g)][:, :, DH * r : DH * (r + 1), :].bitcast(F32), bank)
+
+        def copy_out(copy, sides):
+            copy(out=sides[0], in_=sides[1])
+
 
         def quantise_x(pair):
             tiles = slice(PAIR * pair, PAIR * (pair + 1))
@@ -127,6 +132,14 @@ def tile_groupqueryattention_pa_kernel(
                 out=x_codes[:, tiles].rearrange("p t c m -> p (t c m)").bitcast(FP8X4),
                 scales=x_scales[:, tiles].rearrange("p t c m -> p (t c m)"),
                 in_=grouped[("x", pair)][:].rearrange("p t c m j -> p (t c m j)"),
+            )
+
+        def quantise_w_piece(g, c, heads):
+            cols = slice(DH * heads.start, DH * heads.stop)
+            nc.vector.quantize_mx(
+                out=w_codes[g][:, c, cols].bitcast(FP8X4),
+                scales=w_scales[g][:, c, cols],
+                in_=grouped[("w", g)][:, c, cols, :].rearrange("p n j -> p (n j)"),
             )
 
         def quantise_w(g):
@@ -138,19 +151,14 @@ def tile_groupqueryattention_pa_kernel(
 
         low, high = slice(0, HALF), slice(HALF, DH)
         straight = keep.tile([P, 2, DH], BF16)
-        swapped = keep.tile([P, 2, DH], BF16)
         for which in range(2):
             nc.gpsimd.tensor_copy(out=straight[:, which, :], in_=ident[:])
-            nc.gpsimd.tensor_copy(out=swapped[:, which, low], in_=ident[:, high])
-            nc.gpsimd.tensor_scalar(
-                out=swapped[:, which, high], in0=ident[:, low], scalar1=-1.0, scalar2=0.0, op0=ALU.mult, op1=ALU.add
-            )
-        scaled = keep.tile([P, 2, DH], BF16)
-        scaled_swapped = keep.tile([P, 2, DH], BF16)
+        gain = keep.tile([P, 2, DH], F32)
+        gain_s = keep.tile([P, 2, DH], F32)
         shifted = keep.tile([P, 2, DH], BF16)
         shifted_turned = keep.tile([P, 2, DH], BF16)
 
-        def make_matrices():
+        def make_gains():
             spread = offset_psum.tile([P, 4, DH], F32, name="spread", tag="offset")
             nc.tensor.matmul(
                 out=spread[:].rearrange("p j d -> p (j d)"),
@@ -159,9 +167,16 @@ def tile_groupqueryattention_pa_kernel(
                 start=True,
                 stop=True,
             )
-            scale, shift = spread[:, 0:2, :], spread[:, 2:4, :]
-            nc.vector.tensor_tensor(out=scaled[:], in0=scale, in1=straight[:], op=ALU.mult)
-            nc.vector.tensor_tensor(out=scaled_swapped[:], in0=scale, in1=swapped[:], op=ALU.mult)
+            scale = spread[:, 0:2, :]
+            nc.vector.tensor_scalar_add(out=gain[:], in0=scale, scalar1=1.0)
+            nc.vector.tensor_scalar_add(out=gain_s[:, :, low], in0=scale[:, :, low], scalar1=1.0)
+            nc.vector.tensor_scalar(
+                out=gain_s[:, :, high], in0=scale[:, :, high], scalar1=-1.0, scalar2=-1.0, op0=ALU.mult, op1=ALU.add
+            )
+            return spread
+
+        def make_shift_matrices(spread):
+            shift = spread[:, 2:4, :]
             nc.vector.tensor_tensor(out=shifted[:], in0=shift, in1=straight[:], op=ALU.mult)
             nc.vector.scalar_tensor_tensor(
                 out=shifted_turned[:, :, low],
@@ -176,30 +191,34 @@ def tile_groupqueryattention_pa_kernel(
             )
 
         turned = keep.tile([P, 2, TILES, P], BF16)
-        factors = keep.tile([P, TILES, 2, 2, DH], F32)
+        factors = keep.tile([P, 2, TILES, 2, DH], F32)
 
-        def turn_angles(pair):
-            flipped = flip_psum.tile([P, 2, PAIR, P], BF16, name="angles", tag="flip")
+        def turn_angles(part):
+            flipped = flip_psum.tile([P, 2, BANK_TILES, P], BF16, name="angles", tag="flip")
             for j, table in enumerate((cos_sb, sin_sb)):
-                for i in range(PAIR):
-                    nc.tensor.transpose(flipped[:, j, i, :], table[:, PAIR * pair + i, :], ident_b[:])
-            nc.scalar.copy(out=turned[:, :, PAIR * pair : PAIR * (pair + 1), :], in_=flipped[:])
+                for i in range(BANK_TILES):
+                    nc.tensor.transpose(flipped[:, j, i, :], table[:, BANK_TILES * part + i, :], ident_b[:])
+            nc.scalar.copy(out=turned[:, :, BANK_TILES * part : BANK_TILES * (part + 1), :], in_=flipped[:])
 
-        def make_factors(pair):
-            for t in range(PAIR * pair, PAIR * (pair + 1)):
-                table = flip_psum.tile([P, 2, 2, DH], F32, name="table", tag="flip")
-                for j, terms in enumerate(((straight, scaled), (swapped, scaled_swapped))):
-                    for k, term in enumerate(terms):
-                        nc.tensor.matmul(
-                            out=table[:, j].rearrange("p w d -> p (w d)"),
-                            lhsT=turned[:, j, t, :],
-                            rhs=term[:].rearrange("p w d -> p (w d)"),
-                            start=(k == 0),
-                            stop=(k == 1),
-                        )
-                nc.scalar.copy(out=factors[:, t], in_=table[:])
+        def make_factors(which, pair):
+            tiles = slice(PAIR * pair, PAIR * (pair + 1))
+            out = factors[:, which, tiles]
+            nc.gpsimd.tensor_tensor(
+                out=out[:, :, 0, :],
+                in0=cos_sb[:, tiles, :],
+                in1=gain[:, which, :].unsqueeze(1).to_broadcast([P, PAIR, DH]),
+                op=ALU.mult,
+            )
+            for here, there in ((low, high), (high, low)):
+                nc.gpsimd.tensor_tensor(
+                    out=out[:, :, 1, here],
+                    in0=sin_sb[:, tiles, there],
+                    in1=gain_s[:, which, here].unsqueeze(1).to_broadcast([P, PAIR, HALF]),
+                    op=ALU.mult,
+                )
 
         offsets = {}
+        offset_sb = keep.tile([P, 2, TILES, DH], F32)
 
         def make_offset(which, part):
             offset = offset_psum.tile([P, BANK_TILES, DH], F32, tag="offset")
@@ -213,6 +232,7 @@ def tile_groupqueryattention_pa_kernel(
                         stop=(j == 1),
                     )
             offsets[(which, part)] = offset
+            nc.scalar.copy(out=offset_sb[:, which, BANK_TILES * part : BANK_TILES * (part + 1), :], in_=offset[:])
 
         def project(t, g, acc):
             for c in range(PASSES):
@@ -230,9 +250,9 @@ def tile_groupqueryattention_pa_kernel(
 
         def multiply(acc, t, g, products, i, squares, sum_sq):
             nc.vector.tensor_tensor(
-                out=products[:, i].rearrange("p j (h d) -> p j h d", d=DH),
+                out=products[:, :, :, i, :],
                 in0=acc[:].rearrange("p (h d) -> p h d", d=DH).unsqueeze(1).to_broadcast([P, 2, HEADS, DH]),
-                in1=factors[:, t, :, groups[g][2], :].unsqueeze(2).to_broadcast([P, 2, HEADS, DH]),
+                in1=factors[:, groups[g][2], t].unsqueeze(2).to_broadcast([P, 2, HEADS, DH]),
                 op=ALU.mult,
             )
             for h in range(HEADS):
@@ -248,99 +268,131 @@ def tile_groupqueryattention_pa_kernel(
             return rows[:, :, PAIR * pair : PAIR * (pair + 1), :]
 
         def add_halves(products, stage):
-            straight = products[:, :, 0, :].rearrange("p i (h d) -> p i h d", d=DH)
-            crossed = products[:, :, 1, :].rearrange("p i (h d) -> p i h d", d=DH)
-            rotated = stage[:].rearrange("p h i d -> p i h d")
-            for here, there in ((low, high), (high, low)):
-                nc.gpsimd.tensor_tensor(
-                    out=rotated[:, :, :, here], in0=straight[:, :, :, here], in1=crossed[:, :, :, there], op=ALU.add
+            ahead = products[:, 0].rearrange("p h i (s e) -> p (h i) s e", e=HALF)
+            crossed = products[:, 1].rearrange("p h i (s e) -> p (h i) s e", e=HALF)
+            rotated = stage[:].rearrange("p h i (s e) -> p (h i) s e", e=HALF)
+            nc.gpsimd.tensor_tensor(out=rotated, in0=ahead, in1=crossed[:, :, ::-1, :], op=ALU.add)
+
+        def scale_last(stage, root):
+            i = PAIR - 1
+            for h in range(HEADS):
+                nc.scalar.activation(
+                    out=stage[:, h, i, :],
+                    in_=stage[:, h, i, :],
+                    func=ACT.Copy,
+                    scale=root[:, HEADS * i + h : HEADS * i + h + 1],
                 )
 
-        def finish(g, pair, stage, rms):
+        def finish(g, pair, stage, root, shared):
             which, part = groups[g][2], PAIR * pair // BANK_TILES
             offset = offsets[(which, part)]
-            for i in range(PAIR):
+            for i in range(PAIR - 1 if shared else PAIR):
                 for h in range(HEADS):
                     nc.vector.scalar_tensor_tensor(
                         out=stage[:, h, i, :],
                         in0=stage[:, h, i, :],
-                        scalar=rms[:, HEADS * i + h : HEADS * i + h + 1],
+                        scalar=root[:, HEADS * i + h : HEADS * i + h + 1],
                         in1=offset[:, PAIR * pair + i - BANK_TILES * part, :],
                         op0=ALU.mult,
                         op1=ALU.add,
                     )
+            if shared:
+                last = stage[:, :, PAIR - 1, :]
+                row = offset_sb[:, which, PAIR * pair + PAIR - 1, :]
+                nc.gpsimd.tensor_tensor(
+                    out=last, in0=last, in1=row.unsqueeze(1).to_broadcast([P, HEADS, DH]), op=ALU.add
+                )
             nc.sync.dma_start(out=out_rows(g, pair), in_=stage[:])
 
         def values(pair):
-            stage = stage_pool.tile([P, HEADS, PAIR, DH], F32, name="stage_v")
+            stage = value_pool.tile([P, HEADS, PAIR, DH], F32, name="stage_v")
             for i in range(PAIR):
                 acc = project(PAIR * pair + i, VALUES, flip_psum.tile([P, COLS], F32, name="acc_v", tag="flip"))
                 nc.scalar.copy(out=stage[:, :, i, :], in_=acc[:].rearrange("p (h d) -> p h d", d=DH))
             nc.sync.dma_start(out=out_rows(VALUES, pair), in_=stage[:])
 
-        flip_x(0, 0)
-        flip_x(0, 1, nc.vector.tensor_copy)
-        flip_w(0, 0, nc.scalar.copy, acc_bank)
-        flip_w(0, 1, nc.vector.tensor_copy, acc_bank)
+        copy_out(nc.scalar.copy, flip_x(0, 0))
+        copy_out(nc.vector.tensor_copy, flip_x(0, 1))
+        copy_out(nc.scalar.copy, flip_w(0, 0, acc_bank))
+        copy_out(nc.vector.tensor_copy, flip_w(0, 1, acc_bank))
         quantise_x(0)
-        flip_w(0, 2, nc.scalar.copy, acc_bank)
-        flip_w(0, 3, nc.vector.tensor_copy, acc_bank)
-        make_matrices()
-        turn_angles(0)
-        quantise_w(0)
-        make_factors(0)
+        spread = make_gains()
+        copy_out(nc.scalar.copy, flip_w(0, 2, acc_bank))
+        copy_out(nc.scalar.copy, flip_w(0, 3, acc_bank))
+        for heads in (slice(0, 2), slice(2, 4)):
+            for c in range(PASSES):
+                quantise_w_piece(0, c, heads)
+        for pair in range(PAIRS):
+            make_factors(0, pair)
 
+        rounds = [(g, pair) for g in range(VALUES) for pair in range(PAIRS)]
         flips = {
             0: [("x", 2, 0), ("x", 2, 1), ("w", 1, 0)],
             1: [("x", 3, 0), ("x", 3, 1), ("w", 1, 1)],
             2: [("w", 1, 2), ("w", 1, 3)],
         }
+        by_vector = set([("x", 2, 1), ("x", 3, 1), ("w", 1, 3)])
         for n, g in ((4, 2), (6, VALUES), (8, 3), (12, 4)):
-            flips[n] = [("w", g, 0), ("w", g, 1)]
-            flips[n + 1] = [("w", g, 2), ("w", g, 3)]
+            flips[n - 1] = flips.get(n - 1, []) + [("w", g, 0)]
+            flips[n] = [("w", g, 1), ("w", g, 2)]
+            flips[n + 1] = [("w", g, 3)]
         quantise = {0: ("x", 1), 1: ("x", 2), 2: ("x", 3), 3: ("w", 1), 6: ("w", 2), 8: ("w", VALUES), 10: ("w", 3), 14: ("w", 4)}
-        offset_in = {0: (0, 0), 2: (0, 1), 16: (1, 0), 17: (1, 1)}
+
+        def flip(kind, which, i):
+            return (flip_x if kind == "x" else flip_w)(which, i)
+
+        key_factors_in = {8: 0, 10: 1, 12: 2, 14: 3}
+        offset_in = {0: (0, 0), 3: (0, 1), 16: (1, 0), 17: (1, 1)}
+        shared = set([5, 8, 11, 14])
         values_in = {10: 0, 11: 1, 14: 2, 15: 3}
-        rounds = [(g, pair) for g in range(VALUES) for pair in range(PAIRS)]
 
         def project_round(n):
             g, pair = rounds[n]
             return [project(PAIR * pair + i, g, acc_psum.tile([P, COLS], F32, name="acc", tag="acc")) for i in range(PAIR)]
 
         accs = project_round(0)
-        flip_x(1, 0)
-        flip_x(1, 1)
+        copy_out(nc.scalar.copy, flip_x(1, 0))
+        copy_out(nc.scalar.copy, flip_x(1, 1))
+        turn_angles(0)
         begun = []
-        rms = None
         for n, (g, pair) in enumerate(rounds):
-            products = product_pool.tile([P, PAIR, 2, COLS], F32)
+            products = product_pool.tile([P, 2, HEADS, PAIR, DH], F32)
             sum_sq = small_pool.tile([P, PAIR * HEADS], F32)
             squares = square_pool.tile([P, PAIR * HEADS, DH], F32)
             stage = stage_pool.tile([P, HEADS, PAIR, DH], F32)
+            first = PAIR if n < PAIRS - 1 else 0
+            early, late = flips.get(n, [])[:first], flips.get(n, [])[first:]
+            sides = [flip(*tile) for tile in early]
             multiply(accs[0], PAIR * pair, g, products, 0, squares, sum_sq)
-            if n > 0:
-                nc.vector.reciprocal(out=rms[:], in_=rms[:])
             if n in quantise:
                 kind, which = quantise[n]
                 (quantise_x if kind == "x" else quantise_w)(which)
+            coming = project_round(n + 1) if n + 1 < len(rounds) else None
+            if n == 3:
+                turn_angles(1)
             multiply(accs[1], PAIR * pair + 1, g, products, 1, squares, sum_sq)
-            if n + 1 < len(rounds):
-                accs = project_round(n + 1)
+            accs = coming
             add_halves(products, stage)
-            rms = small_pool.tile([P, PAIR * HEADS], F32)
-            nc.scalar.activation(out=rms[:], in_=sum_sq[:], func=ACT.Sqrt, scale=1.0 / DH, bias=eps[:, 0:1])
-            if n + 1 < PAIRS:
-                turn_angles(n + 1)
-                make_factors(n + 1)
+            if n in key_factors_in:
+                make_factors(1, key_factors_in[n])
+            root = small_pool.tile([P, PAIR * HEADS], F32)
+            nc.scalar.activation(
+                out=root[:], in_=sum_sq[:], func=ACT.Abs_reciprocal_sqrt, scale=1.0 / DH, bias=eps[:, 0:1]
+            )
+            if n > 0 and n - 1 in shared:
+                scale_last(*begun[n - 1][2:4])
+            if n == 0:
+                make_shift_matrices(spread)
             if n in offset_in:
                 make_offset(*offset_in[n])
-            for kind, which, i in flips.get(n, []):
-                (flip_x if kind == "x" else flip_w)(which, i)
-            if n in values_in:
-                values(values_in[n])
-            begun.append((g, pair, stage, rms))
+            begun.append((g, pair, stage, root, n in shared))
             if n >= LAG:
                 finish(*begun[n - LAG])
-        nc.vector.reciprocal(out=rms[:], in_=rms[:])
+            for tile, side in zip(early, sides):
+                copy_out(nc.vector.tensor_copy if tile in by_vector else nc.scalar.copy, side)
+            for tile in late:
+                copy_out(nc.scalar.copy, flip(*tile))
+            if n in values_in:
+                values(values_in[n])
         for n in range(len(rounds) - LAG, len(rounds)):
             finish(*begun[n])

@@ -232,7 +232,10 @@ def tile_groupqueryattention_pa_kernel(
                         stop=(j == 1),
                     )
             offsets[(which, part)] = offset
-            nc.scalar.copy(out=offset_sb[:, which, BANK_TILES * part : BANK_TILES * (part + 1), :], in_=offset[:])
+
+        def copy_offset(which, part):
+            tiles = slice(BANK_TILES * part, BANK_TILES * (part + 1))
+            nc.scalar.copy(out=offset_sb[:, which, tiles, :], in_=offsets[(which, part)][:])
 
         def project(t, g, acc):
             for c in range(PASSES):
@@ -267,10 +270,16 @@ def tile_groupqueryattention_pa_kernel(
             rows = groups[g][1].rearrange("h (p t) d -> p h t d", t=TILES)
             return rows[:, :, PAIR * pair : PAIR * (pair + 1), :]
 
-        def add_halves(products, stage):
-            ahead = products[:, 0].rearrange("p h i (s e) -> p (h i) s e", e=HALF)
-            crossed = products[:, 1].rearrange("p h i (s e) -> p (h i) s e", e=HALF)
-            rotated = stage[:].rearrange("p h i (s e) -> p (h i) s e", e=HALF)
+        def add_halves(products, stage, tiles):
+            if len(tiles) == PAIR:
+                ahead, crossed, rotated = (
+                    view.rearrange("p h i (s e) -> p (h i) s e", e=HALF) for view in (products[:, 0], products[:, 1], stage[:])
+                )
+            else:
+                ahead, crossed, rotated = (
+                    view[:, :, tiles[0], :].rearrange("p h (s e) -> p h s e", e=HALF)
+                    for view in (products[:, 0], products[:, 1], stage[:])
+                )
             nc.gpsimd.tensor_tensor(out=rotated, in0=ahead, in1=crossed[:, :, ::-1, :], op=ALU.add)
 
         def scale_last(stage, root):
@@ -283,7 +292,7 @@ def tile_groupqueryattention_pa_kernel(
                     scale=root[:, HEADS * i + h : HEADS * i + h + 1],
                 )
 
-        def finish(g, pair, stage, root, shared):
+        def finish(g, pair, stage, root, shared, store_apart=False):
             which, part = groups[g][2], PAIR * pair // BANK_TILES
             offset = offsets[(which, part)]
             for i in range(PAIR - 1 if shared else PAIR):
@@ -296,6 +305,10 @@ def tile_groupqueryattention_pa_kernel(
                         op0=ALU.mult,
                         op1=ALU.add,
                     )
+                if not shared and store_apart:
+                    nc.sync.dma_start(out=out_rows(g, pair)[:, :, i, :], in_=stage[:, :, i, :])
+            if store_apart:
+                return
             if shared:
                 last = stage[:, :, PAIR - 1, :]
                 row = offset_sb[:, which, PAIR * pair + PAIR - 1, :]
@@ -336,14 +349,15 @@ def tile_groupqueryattention_pa_kernel(
             flips[n - 1] = flips.get(n - 1, []) + [("w", g, 0)]
             flips[n] = [("w", g, 1), ("w", g, 2)]
             flips[n + 1] = [("w", g, 3)]
-        quantise = {0: ("x", 1), 1: ("x", 2), 2: ("x", 3), 3: ("w", 1), 6: ("w", 2), 8: ("w", VALUES), 10: ("w", 3), 14: ("w", 4)}
+        quantise_x_in = {0: 1, 1: 2, 2: 3}
+        quantise_w_in = {3: 1, 6: 2, 8: VALUES, 10: 3, 14: 4}
 
         def flip(kind, which, i):
             return (flip_x if kind == "x" else flip_w)(which, i)
 
-        key_factors_in = {8: 0, 10: 1, 12: 2, 14: 3}
-        offset_in = {0: (0, 0), 3: (0, 1), 16: (1, 0), 17: (1, 1)}
-        shared = set([5, 8, 11, 14])
+        key_factors_in = {4: 0, 8: 1, 12: 2, 15: 3}
+        offset_in = {0: (0, 0), 1: (0, 1), 16: (1, 0), 17: (1, 1)}
+        shared = set([4, 8, 12])
         values_in = {10: 0, 11: 1, 14: 2, 15: 3}
 
         def project_round(n):
@@ -354,7 +368,14 @@ def tile_groupqueryattention_pa_kernel(
         copy_out(nc.scalar.copy, flip_x(1, 0))
         copy_out(nc.scalar.copy, flip_x(1, 1))
         turn_angles(0)
-        begun = []
+        turn_angles(1)
+
+        def take_root(root, sum_sq):
+            nc.scalar.activation(
+                out=root[:], in_=sum_sq[:], func=ACT.Abs_reciprocal_sqrt, scale=1.0 / DH, bias=eps[:, 0:1]
+            )
+
+        begun, roots = [], []
         for n, (g, pair) in enumerate(rounds):
             products = product_pool.tile([P, 2, HEADS, PAIR, DH], F32)
             sum_sq = small_pool.tile([P, PAIR * HEADS], F32)
@@ -364,21 +385,23 @@ def tile_groupqueryattention_pa_kernel(
             early, late = flips.get(n, [])[:first], flips.get(n, [])[first:]
             sides = [flip(*tile) for tile in early]
             multiply(accs[0], PAIR * pair, g, products, 0, squares, sum_sq)
-            if n in quantise:
-                kind, which = quantise[n]
-                (quantise_x if kind == "x" else quantise_w)(which)
+            last = n == len(rounds) - 1
+            if last:
+                add_halves(products, stage, [0])
+            if n in quantise_x_in:
+                quantise_x(quantise_x_in[n])
+            if n in quantise_w_in:
+                quantise_w(quantise_w_in[n])
             coming = project_round(n + 1) if n + 1 < len(rounds) else None
-            if n == 3:
-                turn_angles(1)
+            if n > 0:
+                take_root(*roots[n - 1])
             multiply(accs[1], PAIR * pair + 1, g, products, 1, squares, sum_sq)
             accs = coming
-            add_halves(products, stage)
+            add_halves(products, stage, [1] if last else [0, 1])
             if n in key_factors_in:
                 make_factors(1, key_factors_in[n])
             root = small_pool.tile([P, PAIR * HEADS], F32)
-            nc.scalar.activation(
-                out=root[:], in_=sum_sq[:], func=ACT.Abs_reciprocal_sqrt, scale=1.0 / DH, bias=eps[:, 0:1]
-            )
+            roots.append((root, sum_sq))
             if n > 0 and n - 1 in shared:
                 scale_last(*begun[n - 1][2:4])
             if n == 0:
@@ -388,11 +411,15 @@ def tile_groupqueryattention_pa_kernel(
             begun.append((g, pair, stage, root, n in shared))
             if n >= LAG:
                 finish(*begun[n - LAG])
+            if n == 4:
+                for part in range(TILES // BANK_TILES):
+                    copy_offset(0, part)
             for tile, side in zip(early, sides):
                 copy_out(nc.vector.tensor_copy if tile in by_vector else nc.scalar.copy, side)
             for tile in late:
                 copy_out(nc.scalar.copy, flip(*tile))
             if n in values_in:
                 values(values_in[n])
+        take_root(*roots[-1])
         for n in range(len(rounds) - LAG, len(rounds)):
-            finish(*begun[n])
+            finish(*begun[n], store_apart=(n == len(rounds) - 1))

@@ -158,7 +158,7 @@ def tile_groupqueryattention_pa_kernel(
         shifted = keep.tile([P, 2, DH], BF16)
         shifted_turned = keep.tile([P, 2, DH], BF16)
 
-        def make_gains():
+        def spread_vectors():
             spread = offset_psum.tile([P, 4, DH], F32, name="spread", tag="offset")
             nc.tensor.matmul(
                 out=spread[:].rearrange("p j d -> p (j d)"),
@@ -167,13 +167,15 @@ def tile_groupqueryattention_pa_kernel(
                 start=True,
                 stop=True,
             )
-            scale = spread[:, 0:2, :]
-            nc.vector.tensor_scalar_add(out=gain[:], in0=scale, scalar1=1.0)
-            nc.vector.tensor_scalar_add(out=gain_s[:, :, low], in0=scale[:, :, low], scalar1=1.0)
-            nc.vector.tensor_scalar(
-                out=gain_s[:, :, high], in0=scale[:, :, high], scalar1=-1.0, scalar2=-1.0, op0=ALU.mult, op1=ALU.add
-            )
             return spread
+
+        def make_gains(spread, which):
+            scale = spread[:, which, :]
+            nc.vector.tensor_scalar_add(out=gain[:, which, :], in0=scale, scalar1=1.0)
+            nc.vector.tensor_scalar_add(out=gain_s[:, which, low], in0=scale[:, low], scalar1=1.0)
+            nc.vector.tensor_scalar(
+                out=gain_s[:, which, high], in0=scale[:, high], scalar1=-1.0, scalar2=-1.0, op0=ALU.mult, op1=ALU.add
+            )
 
         def make_shift_matrices(spread):
             shift = spread[:, 2:4, :]
@@ -327,9 +329,10 @@ def tile_groupqueryattention_pa_kernel(
         copy_out(nc.scalar.copy, flip_x(0, 0))
         copy_out(nc.vector.tensor_copy, flip_x(0, 1))
         copy_out(nc.scalar.copy, flip_w(0, 0, acc_bank))
-        copy_out(nc.vector.tensor_copy, flip_w(0, 1, acc_bank))
+        copy_out(nc.scalar.copy, flip_w(0, 1, acc_bank))
         quantise_x(0)
-        spread = make_gains()
+        spread = spread_vectors()
+        make_gains(spread, 0)
         copy_out(nc.scalar.copy, flip_w(0, 2, acc_bank))
         copy_out(nc.scalar.copy, flip_w(0, 3, acc_bank))
         for heads in (slice(0, 2), slice(2, 4)):
@@ -355,9 +358,9 @@ def tile_groupqueryattention_pa_kernel(
         def flip(kind, which, i):
             return (flip_x if kind == "x" else flip_w)(which, i)
 
-        key_factors_in = {4: 0, 8: 1, 12: 2, 15: 3}
+        key_factors_in = {3: 0, 4: 1, 11: 2, 13: 3}
         offset_in = {0: (0, 0), 1: (0, 1), 16: (1, 0), 17: (1, 1)}
-        shared = set([4, 8, 12])
+        shared = set(range(4, 16, 2))
         values_in = {10: 0, 11: 1, 14: 2, 15: 3}
 
         def project_round(n):
@@ -402,9 +405,8 @@ def tile_groupqueryattention_pa_kernel(
                 make_factors(1, key_factors_in[n])
             root = small_pool.tile([P, PAIR * HEADS], F32)
             roots.append((root, sum_sq))
-            if n > 0 and n - 1 in shared:
-                scale_last(*begun[n - 1][2:4])
             if n == 0:
+                make_gains(spread, 1)
                 make_shift_matrices(spread)
             if n in offset_in:
                 make_offset(*offset_in[n])
@@ -418,6 +420,8 @@ def tile_groupqueryattention_pa_kernel(
                 copy_out(nc.vector.tensor_copy if tile in by_vector else nc.scalar.copy, side)
             for tile in late:
                 copy_out(nc.scalar.copy, flip(*tile))
+            if n > 0 and n - 1 in shared:
+                scale_last(*begun[n - 1][2:4])
             if n in values_in:
                 values(values_in[n])
         take_root(*roots[-1])

@@ -153,8 +153,15 @@ def tile_groupqueryattention_pa_kernel(
         straight = keep.tile([P, 2, DH], BF16)
         for which in range(2):
             nc.gpsimd.tensor_copy(out=straight[:, which, :], in_=ident[:])
-        gain = keep.tile([P, 2, DH], F32)
-        gain_s = keep.tile([P, 2, DH], F32)
+        turning = keep.tile([P, DH], BF16)
+        nc.gpsimd.tensor_copy(out=turning[:, low], in_=ident[:, high])
+        nc.gpsimd.tensor_scalar(
+            out=turning[:, high], in0=ident[:, low], scalar1=-1.0, scalar2=0.0, op0=ALU.mult, op1=ALU.add
+        )
+        gain = keep.tile([P, DH], F32)
+        gain_s = keep.tile([P, DH], F32)
+        scaled = keep.tile([P, DH], BF16)
+        scaled_turning = keep.tile([P, DH], BF16)
         shifted = keep.tile([P, 2, DH], BF16)
         shifted_turned = keep.tile([P, 2, DH], BF16)
 
@@ -169,13 +176,18 @@ def tile_groupqueryattention_pa_kernel(
             )
             return spread
 
-        def make_gains(spread, which):
-            scale = spread[:, which, :]
-            nc.vector.tensor_scalar_add(out=gain[:, which, :], in0=scale, scalar1=1.0)
-            nc.vector.tensor_scalar_add(out=gain_s[:, which, low], in0=scale[:, low], scalar1=1.0)
+        def make_gains(spread):
+            scale = spread[:, 0, :]
+            nc.vector.tensor_scalar_add(out=gain[:], in0=scale, scalar1=1.0)
+            nc.vector.tensor_scalar_add(out=gain_s[:, low], in0=scale[:, low], scalar1=1.0)
             nc.vector.tensor_scalar(
-                out=gain_s[:, which, high], in0=scale[:, high], scalar1=-1.0, scalar2=-1.0, op0=ALU.mult, op1=ALU.add
+                out=gain_s[:, high], in0=scale[:, high], scalar1=-1.0, scalar2=-1.0, op0=ALU.mult, op1=ALU.add
             )
+
+        def make_scale_matrices(spread):
+            scale = spread[:, 1, :]
+            nc.vector.tensor_tensor(out=scaled[:], in0=scale, in1=straight[:, 0, :], op=ALU.mult)
+            nc.vector.tensor_tensor(out=scaled_turning[:], in0=scale, in1=turning[:], op=ALU.mult)
 
         def make_shift_matrices(spread):
             shift = spread[:, 2:4, :]
@@ -202,25 +214,38 @@ def tile_groupqueryattention_pa_kernel(
                     nc.tensor.transpose(flipped[:, j, i, :], table[:, BANK_TILES * part + i, :], ident_b[:])
             nc.scalar.copy(out=turned[:, :, BANK_TILES * part : BANK_TILES * (part + 1), :], in_=flipped[:])
 
-        def make_factors(which, pair):
+        def make_query_factors(pair):
             tiles = slice(PAIR * pair, PAIR * (pair + 1))
-            out = factors[:, which, tiles]
+            out = factors[:, 0, tiles]
             nc.gpsimd.tensor_tensor(
                 out=out[:, :, 0, :],
                 in0=cos_sb[:, tiles, :],
-                in1=gain[:, which, :].unsqueeze(1).to_broadcast([P, PAIR, DH]),
+                in1=gain[:].unsqueeze(1).to_broadcast([P, PAIR, DH]),
                 op=ALU.mult,
             )
             for here, there in ((low, high), (high, low)):
                 nc.gpsimd.tensor_tensor(
                     out=out[:, :, 1, here],
                     in0=sin_sb[:, tiles, there],
-                    in1=gain_s[:, which, here].unsqueeze(1).to_broadcast([P, PAIR, HALF]),
+                    in1=gain_s[:, here].unsqueeze(1).to_broadcast([P, PAIR, HALF]),
                     op=ALU.mult,
                 )
 
+        def make_key_factors(pair):
+            table = flip_psum.tile([P, PAIR, 2, DH], F32, name="table", tag="flip")
+            for i in range(PAIR):
+                for j, terms in enumerate(((straight[:, 0, :], scaled[:]), (turning[:], scaled_turning[:]))):
+                    for k, term in enumerate(terms):
+                        nc.tensor.matmul(
+                            out=table[:, i, j, :],
+                            lhsT=turned[:, j, PAIR * pair + i, :],
+                            rhs=term,
+                            start=(k == 0),
+                            stop=(k == 1),
+                        )
+            nc.scalar.copy(out=factors[:, 1, PAIR * pair : PAIR * (pair + 1)], in_=table[:])
+
         offsets = {}
-        offset_sb = keep.tile([P, 2, TILES, DH], F32)
 
         def make_offset(which, part):
             offset = offset_psum.tile([P, BANK_TILES, DH], F32, tag="offset")
@@ -234,10 +259,6 @@ def tile_groupqueryattention_pa_kernel(
                         stop=(j == 1),
                     )
             offsets[(which, part)] = offset
-
-        def copy_offset(which, part):
-            tiles = slice(BANK_TILES * part, BANK_TILES * (part + 1))
-            nc.scalar.copy(out=offset_sb[:, which, tiles, :], in_=offsets[(which, part)][:])
 
         def project(t, g, acc):
             for c in range(PASSES):
@@ -284,40 +305,43 @@ def tile_groupqueryattention_pa_kernel(
                 )
             nc.gpsimd.tensor_tensor(out=rotated, in0=ahead, in1=crossed[:, :, ::-1, :], op=ALU.add)
 
-        def scale_last(stage, root):
-            i = PAIR - 1
-            for h in range(HEADS):
-                nc.scalar.activation(
-                    out=stage[:, h, i, :],
-                    in_=stage[:, h, i, :],
-                    func=ACT.Copy,
-                    scale=root[:, HEADS * i + h : HEADS * i + h + 1],
-                )
+        def scale_all(stage, root):
+            for i in range(PAIR):
+                for h in range(HEADS):
+                    nc.scalar.activation(
+                        out=stage[:, h, i, :],
+                        in_=stage[:, h, i, :],
+                        func=ACT.Copy,
+                        scale=root[:, HEADS * i + h : HEADS * i + h + 1],
+                    )
 
         def finish(g, pair, stage, root, shared, store_apart=False):
             which, part = groups[g][2], PAIR * pair // BANK_TILES
-            offset = offsets[(which, part)]
-            for i in range(PAIR - 1 if shared else PAIR):
+            first = PAIR * pair - BANK_TILES * part
+            offset = offsets[(which, part)][:, first : first + PAIR, :]
+            if shared:
+                nc.vector.tensor_tensor(
+                    out=stage[:],
+                    in0=stage[:],
+                    in1=offset.unsqueeze(1).to_broadcast([P, HEADS, PAIR, DH]),
+                    op=ALU.add,
+                )
+                nc.sync.dma_start(out=out_rows(g, pair), in_=stage[:])
+                return
+            for i in range(PAIR):
                 for h in range(HEADS):
                     nc.vector.scalar_tensor_tensor(
                         out=stage[:, h, i, :],
                         in0=stage[:, h, i, :],
                         scalar=root[:, HEADS * i + h : HEADS * i + h + 1],
-                        in1=offset[:, PAIR * pair + i - BANK_TILES * part, :],
+                        in1=offset[:, i, :],
                         op0=ALU.mult,
                         op1=ALU.add,
                     )
-                if not shared and store_apart:
+                if store_apart:
                     nc.sync.dma_start(out=out_rows(g, pair)[:, :, i, :], in_=stage[:, :, i, :])
-            if store_apart:
-                return
-            if shared:
-                last = stage[:, :, PAIR - 1, :]
-                row = offset_sb[:, which, PAIR * pair + PAIR - 1, :]
-                nc.gpsimd.tensor_tensor(
-                    out=last, in0=last, in1=row.unsqueeze(1).to_broadcast([P, HEADS, DH]), op=ALU.add
-                )
-            nc.sync.dma_start(out=out_rows(g, pair), in_=stage[:])
+            if not store_apart:
+                nc.sync.dma_start(out=out_rows(g, pair), in_=stage[:])
 
         def values(pair):
             stage = value_pool.tile([P, HEADS, PAIR, DH], F32, name="stage_v")
@@ -332,14 +356,14 @@ def tile_groupqueryattention_pa_kernel(
         copy_out(nc.scalar.copy, flip_w(0, 1, acc_bank))
         quantise_x(0)
         spread = spread_vectors()
-        make_gains(spread, 0)
+        make_gains(spread)
         copy_out(nc.scalar.copy, flip_w(0, 2, acc_bank))
         copy_out(nc.scalar.copy, flip_w(0, 3, acc_bank))
         for heads in (slice(0, 2), slice(2, 4)):
             for c in range(PASSES):
                 quantise_w_piece(0, c, heads)
         for pair in range(PAIRS):
-            make_factors(0, pair)
+            make_query_factors(pair)
 
         rounds = [(g, pair) for g in range(VALUES) for pair in range(PAIRS)]
         flips = {
@@ -358,9 +382,9 @@ def tile_groupqueryattention_pa_kernel(
         def flip(kind, which, i):
             return (flip_x if kind == "x" else flip_w)(which, i)
 
-        key_factors_in = {3: 0, 4: 1, 11: 2, 13: 3}
+        key_factors_in = {4: 0, 8: 1, 12: 2, 15: 3}
         offset_in = {0: (0, 0), 1: (0, 1), 16: (1, 0), 17: (1, 1)}
-        shared = set(range(4, 16, 2))
+        shared = set([4, 6, 8, 10, 12, 14, 15, 16, 17, 18])
         values_in = {10: 0, 11: 1, 14: 2, 15: 3}
 
         def project_round(n):
@@ -402,26 +426,23 @@ def tile_groupqueryattention_pa_kernel(
             accs = coming
             add_halves(products, stage, [1] if last else [0, 1])
             if n in key_factors_in:
-                make_factors(1, key_factors_in[n])
+                make_key_factors(key_factors_in[n])
             root = small_pool.tile([P, PAIR * HEADS], F32)
             roots.append((root, sum_sq))
             if n == 0:
-                make_gains(spread, 1)
+                make_scale_matrices(spread)
                 make_shift_matrices(spread)
             if n in offset_in:
                 make_offset(*offset_in[n])
             begun.append((g, pair, stage, root, n in shared))
             if n >= LAG:
                 finish(*begun[n - LAG])
-            if n == 4:
-                for part in range(TILES // BANK_TILES):
-                    copy_offset(0, part)
             for tile, side in zip(early, sides):
                 copy_out(nc.vector.tensor_copy if tile in by_vector else nc.scalar.copy, side)
             for tile in late:
                 copy_out(nc.scalar.copy, flip(*tile))
             if n > 0 and n - 1 in shared:
-                scale_last(*begun[n - 1][2:4])
+                scale_all(*begun[n - 1][2:4])
             if n in values_in:
                 values(values_in[n])
         take_root(*roots[-1])

@@ -246,6 +246,7 @@ def tile_groupqueryattention_pa_kernel(
             nc.scalar.copy(out=factors[:, 1, PAIR * pair : PAIR * (pair + 1)], in_=table[:])
 
         offsets = {}
+        offset_sb = keep.tile([P, 2, TILES, DH], F32)
 
         def make_offset(which, part):
             offset = offset_psum.tile([P, BANK_TILES, DH], F32, tag="offset")
@@ -259,6 +260,10 @@ def tile_groupqueryattention_pa_kernel(
                         stop=(j == 1),
                     )
             offsets[(which, part)] = offset
+
+        def copy_offset(which, part):
+            tiles = slice(BANK_TILES * part, BANK_TILES * (part + 1))
+            nc.scalar.copy(out=offset_sb[:, which, tiles, :], in_=offsets[(which, part)][:])
 
         def project(t, g, acc):
             for c in range(PASSES):
@@ -293,55 +298,49 @@ def tile_groupqueryattention_pa_kernel(
             rows = groups[g][1].rearrange("h (p t) d -> p h t d", t=TILES)
             return rows[:, :, PAIR * pair : PAIR * (pair + 1), :]
 
-        def add_halves(products, stage, tiles):
-            if len(tiles) == PAIR:
-                ahead, crossed, rotated = (
-                    view.rearrange("p h i (s e) -> p (h i) s e", e=HALF) for view in (products[:, 0], products[:, 1], stage[:])
+        def add_halves(products, stage):
+            ahead, crossed, rotated = (
+                view.rearrange("p h i d -> p (h i) d") for view in (products[:, 0], products[:, 1], stage[:])
+            )
+            for here, there in ((low, high), (high, low)):
+                nc.gpsimd.tensor_tensor(
+                    out=rotated[:, :, here], in0=ahead[:, :, here], in1=crossed[:, :, there], op=ALU.add
                 )
-            else:
-                ahead, crossed, rotated = (
-                    view[:, :, tiles[0], :].rearrange("p h (s e) -> p h s e", e=HALF)
-                    for view in (products[:, 0], products[:, 1], stage[:])
-                )
-            nc.gpsimd.tensor_tensor(out=rotated, in0=ahead, in1=crossed[:, :, ::-1, :], op=ALU.add)
 
-        def scale_all(stage, root):
-            for i in range(PAIR):
-                for h in range(HEADS):
-                    nc.scalar.activation(
-                        out=stage[:, h, i, :],
-                        in_=stage[:, h, i, :],
-                        func=ACT.Copy,
-                        scale=root[:, HEADS * i + h : HEADS * i + h + 1],
-                    )
+        def scale_last(stage, root):
+            i = PAIR - 1
+            for h in range(HEADS):
+                nc.scalar.activation(
+                    out=stage[:, h, i, :],
+                    in_=stage[:, h, i, :],
+                    func=ACT.Copy,
+                    scale=root[:, HEADS * i + h : HEADS * i + h + 1],
+                )
 
         def finish(g, pair, stage, root, shared, store_apart=False):
             which, part = groups[g][2], PAIR * pair // BANK_TILES
-            first = PAIR * pair - BANK_TILES * part
-            offset = offsets[(which, part)][:, first : first + PAIR, :]
-            if shared:
-                nc.vector.tensor_tensor(
-                    out=stage[:],
-                    in0=stage[:],
-                    in1=offset.unsqueeze(1).to_broadcast([P, HEADS, PAIR, DH]),
-                    op=ALU.add,
-                )
-                nc.sync.dma_start(out=out_rows(g, pair), in_=stage[:])
-                return
-            for i in range(PAIR):
+            offset = offsets[(which, part)]
+            for i in range(PAIR - 1 if shared else PAIR):
                 for h in range(HEADS):
                     nc.vector.scalar_tensor_tensor(
                         out=stage[:, h, i, :],
                         in0=stage[:, h, i, :],
                         scalar=root[:, HEADS * i + h : HEADS * i + h + 1],
-                        in1=offset[:, i, :],
+                        in1=offset[:, PAIR * pair + i - BANK_TILES * part, :],
                         op0=ALU.mult,
                         op1=ALU.add,
                     )
-                if store_apart:
+                if not shared and store_apart:
                     nc.sync.dma_start(out=out_rows(g, pair)[:, :, i, :], in_=stage[:, :, i, :])
-            if not store_apart:
-                nc.sync.dma_start(out=out_rows(g, pair), in_=stage[:])
+            if store_apart:
+                return
+            if shared:
+                last = stage[:, :, PAIR - 1, :]
+                row = offset_sb[:, which, PAIR * pair + PAIR - 1, :]
+                nc.gpsimd.tensor_tensor(
+                    out=last, in0=last, in1=row.unsqueeze(1).to_broadcast([P, HEADS, DH]), op=ALU.add
+                )
+            nc.sync.dma_start(out=out_rows(g, pair), in_=stage[:])
 
         def values(pair):
             stage = value_pool.tile([P, HEADS, PAIR, DH], F32, name="stage_v")
@@ -382,9 +381,9 @@ def tile_groupqueryattention_pa_kernel(
         def flip(kind, which, i):
             return (flip_x if kind == "x" else flip_w)(which, i)
 
-        key_factors_in = {4: 0, 8: 1, 12: 2, 15: 3}
+        key_factors_in = {14: 0, 15: 1, 16: 2, 17: 3}
         offset_in = {0: (0, 0), 1: (0, 1), 16: (1, 0), 17: (1, 1)}
-        shared = set([4, 6, 8, 10, 12, 14, 15, 16, 17, 18])
+        shared = set([4, 8, 12])
         values_in = {10: 0, 11: 1, 14: 2, 15: 3}
 
         def project_round(n):
@@ -412,9 +411,6 @@ def tile_groupqueryattention_pa_kernel(
             early, late = flips.get(n, [])[:first], flips.get(n, [])[first:]
             sides = [flip(*tile) for tile in early]
             multiply(accs[0], PAIR * pair, g, products, 0, squares, sum_sq)
-            last = n == len(rounds) - 1
-            if last:
-                add_halves(products, stage, [0])
             if n in quantise_x_in:
                 quantise_x(quantise_x_in[n])
             if n in quantise_w_in:
@@ -424,7 +420,7 @@ def tile_groupqueryattention_pa_kernel(
                 take_root(*roots[n - 1])
             multiply(accs[1], PAIR * pair + 1, g, products, 1, squares, sum_sq)
             accs = coming
-            add_halves(products, stage, [1] if last else [0, 1])
+            add_halves(products, stage)
             if n in key_factors_in:
                 make_key_factors(key_factors_in[n])
             root = small_pool.tile([P, PAIR * HEADS], F32)
@@ -437,12 +433,15 @@ def tile_groupqueryattention_pa_kernel(
             begun.append((g, pair, stage, root, n in shared))
             if n >= LAG:
                 finish(*begun[n - LAG])
+            if n == 4:
+                for part in range(TILES // BANK_TILES):
+                    copy_offset(0, part)
             for tile, side in zip(early, sides):
                 copy_out(nc.vector.tensor_copy if tile in by_vector else nc.scalar.copy, side)
             for tile in late:
                 copy_out(nc.scalar.copy, flip(*tile))
             if n > 0 and n - 1 in shared:
-                scale_all(*begun[n - 1][2:4])
+                scale_last(*begun[n - 1][2:4])
             if n in values_in:
                 values(values_in[n])
         take_root(*roots[-1])

@@ -43,9 +43,9 @@ def tile_groupqueryattention_pa_kernel(
         value_pool = ctx.enter_context(tc.tile_pool(name="values", bufs=2))
         square_pool = ctx.enter_context(tc.tile_pool(name="squares", bufs=2))
         small_pool = ctx.enter_context(tc.tile_pool(name="small", bufs=LAG + 3))
-        flip_psum = ctx.enter_context(tc.psum_pool(name="flip", bufs=2))
+        flip_psum = ctx.enter_context(tc.psum_pool(name="flip", bufs=3))
         offset_psum = ctx.enter_context(tc.psum_pool(name="offset", bufs=2))
-        acc_psum = ctx.enter_context(tc.psum_pool(name="acc", bufs=4))
+        acc_psum = ctx.enter_context(tc.psum_pool(name="acc", bufs=3))
         ctx.enter_context(tc.manual_schedule())
 
         groups = [(wq[COLS * g : COLS * (g + 1), :], out_0[0, HEADS * g : HEADS * (g + 1)], 0) for g in range(4)]
@@ -351,7 +351,7 @@ def tile_groupqueryattention_pa_kernel(
 
         copy_out(nc.scalar.copy, flip_x(0, 0))
         copy_out(nc.vector.tensor_copy, flip_x(0, 1))
-        copy_out(nc.scalar.copy, flip_w(0, 0, acc_bank))
+        copy_out(nc.scalar.copy, flip_w(0, 0))
         copy_out(nc.scalar.copy, flip_w(0, 1, acc_bank))
         quantise_x(0)
         spread = spread_vectors()
@@ -370,7 +370,7 @@ def tile_groupqueryattention_pa_kernel(
             1: [("x", 3, 0), ("x", 3, 1), ("w", 1, 1)],
             2: [("w", 1, 2), ("w", 1, 3)],
         }
-        by_vector = set([("x", 2, 1), ("x", 3, 1), ("w", 1, 3)])
+        by_vector = set([("x", 2, 1), ("x", 3, 1)])
         for n, g in ((4, 2), (6, VALUES), (8, 3), (12, 4)):
             flips[n - 1] = flips.get(n - 1, []) + [("w", g, 0)]
             flips[n] = [("w", g, 1), ("w", g, 2)]
@@ -382,16 +382,16 @@ def tile_groupqueryattention_pa_kernel(
             return (flip_x if kind == "x" else flip_w)(which, i)
 
         key_factors_in = {14: 0, 15: 1, 16: 2, 17: 3}
-        offset_in = {0: (0, 0), 1: (0, 1), 16: (1, 0), 17: (1, 1)}
+        offset_in = {0: (0, 0), 1: (0, 1), 16: (1, 0), 18: (1, 1)}
         shared = set([4, 8, 12])
         values_in = {10: 0, 11: 1, 14: 2, 15: 3}
 
-        def project_round(n):
+        def project_tile(n, i):
             g, pair = rounds[n]
-            return [project(PAIR * pair + i, g, acc_psum.tile([P, COLS], F32, name="acc", tag="acc")) for i in range(PAIR)]
+            return project(PAIR * pair + i, g, acc_psum.tile([P, COLS], F32, name="acc", tag="acc"))
 
-        accs = project_round(0)
         copy_out(nc.scalar.copy, flip_x(1, 0))
+        accs = [project_tile(0, i) for i in range(PAIR)]
         copy_out(nc.scalar.copy, flip_x(1, 1))
         turn_angles(0)
         turn_angles(1)
@@ -415,11 +415,11 @@ def tile_groupqueryattention_pa_kernel(
                 quantise_x(quantise_x_in[n])
             if n in quantise_w_in:
                 quantise_w(quantise_w_in[n])
-            coming = project_round(n + 1) if n + 1 < len(rounds) else None
+            more = n + 1 < len(rounds)
+            coming = [project_tile(n + 1, 0)] if more else []
             if n > 0:
                 take_root(*roots[n - 1])
             multiply(accs[1], PAIR * pair + 1, g, products, 1, squares, sum_sq)
-            accs = coming
             add_halves(products, stage)
             if n in key_factors_in:
                 make_key_factors(key_factors_in[n])
@@ -428,8 +428,6 @@ def tile_groupqueryattention_pa_kernel(
             if n == 0:
                 make_scale_matrices(spread)
                 make_shift_matrices(spread)
-            if n in offset_in:
-                make_offset(*offset_in[n])
             begun.append((g, pair, stage, root, n in shared))
             if n >= LAG:
                 finish(*begun[n - LAG])
@@ -440,6 +438,11 @@ def tile_groupqueryattention_pa_kernel(
                 copy_out(nc.vector.tensor_copy if tile in by_vector else nc.scalar.copy, side)
             for tile in late:
                 copy_out(nc.scalar.copy, flip(*tile))
+            if more:
+                coming.append(project_tile(n + 1, 1))
+            accs = coming
+            if n in offset_in:
+                make_offset(*offset_in[n])
             if n > 0 and n - 1 in shared:
                 scale_last(*begun[n - 1][2:4])
             if n in values_in:

from contextlib import ExitStack

import concourse.mybir as mybir
from concourse.masks import make_identity

F32 = mybir.dt.float32
BF16 = mybir.dt.bfloat16
U32 = mybir.dt.uint32
U8 = mybir.dt.uint8
FP8X4 = mybir.dt.float8_e4m3fn_x4
ALU = mybir.AluOpType
ACT = mybir.ActivationFunctionType

P = 128
S = 1024
D = 1024
DH = 128
HALF = DH // 2
EPS = 1e-6
TILES = S // P
PACK = 4
PASSES = D // (P * PACK)
CHUNKS = D // 2 // P
HEADS = 4
COLS = HEADS * DH
PAIR = 2
PAIRS = TILES // PAIR
BANK_TILES = 512 // DH
LAG = 2

FLOPS = 2 * S * D * (16 + 4 + 4) * DH


def tile_groupqueryattention_pa_kernel(
    tc, x, sin_thetas, cos_thetas, wq, wk, wv, q_scale, q_shift, k_scale, k_shift, out_0, out_1, out_2
):
    nc = tc.nc
    with ExitStack() as ctx:
        keep = ctx.enter_context(tc.tile_pool(name="keep", bufs=1))
        grouped_pool = ctx.enter_context(tc.tile_pool(name="grouped", bufs=2))
        product_pool = ctx.enter_context(tc.tile_pool(name="products", bufs=3))
        stage_pool = ctx.enter_context(tc.tile_pool(name="stage", bufs=LAG + 3))
        value_pool = ctx.enter_context(tc.tile_pool(name="values", bufs=2))
        square_pool = ctx.enter_context(tc.tile_pool(name="squares", bufs=2))
        small_pool = ctx.enter_context(tc.tile_pool(name="small", bufs=LAG + 3))
        flip_psum = ctx.enter_context(tc.psum_pool(name="flip", bufs=3))
        offset_psum = ctx.enter_context(tc.psum_pool(name="offset", bufs=2))
        acc_psum = ctx.enter_context(tc.psum_pool(name="acc", bufs=3))
        ctx.enter_context(tc.manual_schedule())

        groups = [(wq[COLS * g : COLS * (g + 1), :], out_0[0, HEADS * g : HEADS * (g + 1)], 0) for g in range(4)]
        groups.append((wk, out_1[0], 1))
        VALUES = len(groups)
        groups.append((wv, out_2[0], None))

        vectors = keep.tile([P, 4, DH], BF16)
        nc.vector.memset(vectors[:], 0.0)
        for j, vector in enumerate((q_scale, k_scale, q_shift, k_shift)):
            nc.scalar.dma_start(out=vectors[0:1, j, :], in_=vector.unsqueeze(0))

        x_sb = keep.tile([P, TILES, D], BF16)
        x_view = x[0].rearrange("(p t) d -> p t d", t=TILES)
        w_sb = [keep.tile([P, HEADS, D], BF16, name="w_sb%d" % g) for g in range(len(groups))]
        cos_sb = keep.tile([P, TILES, DH], BF16)
        sin_sb = keep.tile([P, TILES, DH], BF16)

        def load_x(pair):
            tiles = slice(PAIR * pair, PAIR * (pair + 1))
            nc.sync.dma_start(out=x_sb[:, tiles, :], in_=x_view[:, tiles, :])

        def load_w(g, rows=slice(0, HEADS)):
            nc.sync.dma_start(out=w_sb[g][:, rows, :], in_=groups[g][0].rearrange("(r p) i -> p r i", p=P)[:, rows, :])

        load_x(0)
        load_w(0, slice(0, 2))
        load_w(0, slice(2, 4))
        nc.sync.dma_start(out=cos_sb[:], in_=cos_thetas.rearrange("(p t) d -> p t d", t=TILES))
        nc.sync.dma_start(out=sin_sb[:], in_=sin_thetas.rearrange("(p t) d -> p t d", t=TILES))
        for pair in range(1, PAIRS):
            load_x(pair)
        for g in (1, 2, VALUES, 3, 4):
            load_w(g)

        eps = keep.tile([P, 1], F32)
        nc.vector.memset(eps[:], EPS)
        ones = keep.tile([P, P], BF16)
        nc.vector.memset(ones[:], 1.0)
        first_root = keep.tile([P, 1], F32)
        nc.scalar.activation(out=first_root[:], in_=eps[:], func=ACT.Abs_reciprocal_sqrt)
        ident = keep.tile([P, P], F32)
        make_identity(nc, ident[:])
        ident_b = keep.tile([P, P], BF16)
        nc.vector.tensor_copy(out=ident_b[:], in_=ident[:])

        def flip_rows(rows, grouped_words, bank):
            words = rows.bitcast(F32)
            flipped = bank()
            for piece in range(CHUNKS):
                c, u = divmod(piece, 2)
                nc.tensor.transpose(flipped[:, piece, :], words[:, 2 * P * c + u : 2 * P * (c + 1) : 2], ident[:])
            return grouped_words, flipped[:].rearrange("p (c u) n -> p c n u", u=2)

        def flip_bank():
            return flip_psum.tile([P, CHUNKS, P], F32, name="flipped", tag="flip")

        def acc_bank():
            return acc_psum.tile([P, CHUNKS, P], F32, name="flipped_early", tag="acc")

        x_codes = keep.tile([P, TILES, PASSES, P], U32, align_bytes=64)
        x_scales = keep.tile([P, TILES, PASSES, P], U8, align_bytes=64)
        w_codes = [keep.tile([P, PASSES, COLS], U32, align_bytes=64, name="w_codes%d" % g) for g in range(len(groups))]
        w_scales = [keep.tile([P, PASSES, COLS], U8, align_bytes=64, name="w_scales%d" % g) for g in range(len(groups))]
        grouped = {}

        def flip_x(pair, i, bank=flip_bank):
            if ("x", pair) not in grouped:
                grouped[("x", pair)] = grouped_pool.tile([P, PAIR, PASSES, P, PACK], BF16, align_bytes=64, name="x_grouped")
            return flip_rows(x_sb[:, PAIR * pair + i, :], grouped[("x", pair)][:, i].bitcast(F32), bank)

        def flip_w(g, r, bank=flip_bank):
            if ("w", g) not in grouped:
                grouped[("w", g)] = grouped_pool.tile([P, PASSES, COLS, PACK], BF16, align_bytes=64, name="w_grouped")
            return flip_rows(w_sb[g][:, r, :], grouped[("w", g)][:, :, DH * r : DH * (r + 1), :].bitcast(F32), bank)

        def copy_out(copy, sides):
            copy(out=sides[0], in_=sides[1])


        def quantise_x(pair):
            tiles = slice(PAIR * pair, PAIR * (pair + 1))
            nc.vector.quantize_mx(
                out=x_codes[:, tiles].rearrange("p t c m -> p (t c m)").bitcast(FP8X4),
                scales=x_scales[:, tiles].rearrange("p t c m -> p (t c m)"),
                in_=grouped[("x", pair)][:].rearrange("p t c m j -> p (t c m j)"),
            )

        def quantise_w_piece(g, c, heads):
            cols = slice(DH * heads.start, DH * heads.stop)
            nc.vector.quantize_mx(
                out=w_codes[g][:, c, cols].bitcast(FP8X4),
                scales=w_scales[g][:, c, cols],
                in_=grouped[("w", g)][:, c, cols, :].rearrange("p n j -> p (n j)"),
            )

        def quantise_w(g):
            nc.vector.quantize_mx(
                out=w_codes[g][:].rearrange("p c n -> p (c n)").bitcast(FP8X4),
                scales=w_scales[g][:].rearrange("p c n -> p (c n)"),
                in_=grouped[("w", g)][:].rearrange("p c n j -> p (c n j)"),
            )

        low, high = slice(0, HALF), slice(HALF, DH)
        straight = keep.tile([P, 2, DH], BF16)
        for which in range(2):
            nc.gpsimd.tensor_copy(out=straight[:, which, :], in_=ident[:])
        turning = keep.tile([P, DH], BF16)
        nc.gpsimd.tensor_copy(out=turning[:, low], in_=ident[:, high])
        nc.gpsimd.tensor_scalar(
            out=turning[:, high], in0=ident[:, low], scalar1=-1.0, scalar2=0.0, op0=ALU.mult, op1=ALU.add
        )
        gain = keep.tile([P, DH], F32)
        gain_s = keep.tile([P, DH], F32)
        scaled = keep.tile([P, DH], BF16)
        scaled_turning = keep.tile([P, DH], BF16)
        shifted = keep.tile([P, 2, DH], BF16)
        shifted_turned = keep.tile([P, 2, DH], BF16)

        def spread_vectors():
            spread = offset_psum.tile([P, 4, DH], F32, name="spread", tag="offset")
            nc.tensor.matmul(
                out=spread[:].rearrange("p j d -> p (j d)"),
                lhsT=ones[:],
                rhs=vectors[:].rearrange("p j d -> p (j d)"),
                start=True,
                stop=True,
            )
            return spread

        def make_gains(spread):
            scale = spread[:, 0, :]
            nc.vector.tensor_scalar_add(out=gain[:], in0=scale, scalar1=1.0)
            nc.vector.tensor_scalar_add(out=gain_s[:, low], in0=scale[:, low], scalar1=1.0)
            nc.vector.tensor_scalar(
                out=gain_s[:, high], in0=scale[:, high], scalar1=-1.0, scalar2=-1.0, op0=ALU.mult, op1=ALU.add
            )

        def make_scale_matrices(spread):
            scale = spread[:, 1, :]
            nc.vector.tensor_tensor(out=scaled[:], in0=scale, in1=straight[:, 0, :], op=ALU.mult)
            nc.vector.tensor_tensor(out=scaled_turning[:], in0=scale, in1=turning[:], op=ALU.mult)

        def make_shift_matrices(spread):
            shift = spread[:, 2:4, :]
            nc.vector.tensor_tensor(out=shifted[:], in0=shift, in1=straight[:], op=ALU.mult)
            nc.vector.scalar_tensor_tensor(
                out=shifted_turned[:, :, low],
                in0=shift[:, :, high],
                scalar=-1.0,
                in1=straight[:, :, low],
                op0=ALU.mult,
                op1=ALU.mult,
            )
            nc.vector.tensor_tensor(
                out=shifted_turned[:, :, high], in0=shift[:, :, low], in1=straight[:, :, high], op=ALU.mult
            )

        turned = keep.tile([P, 2, TILES, P], BF16)
        factors = keep.tile([P, 2, TILES, 2, DH], F32)

        def turn_angles(part):
            flipped = flip_psum.tile([P, 2, BANK_TILES, P], BF16, name="angles", tag="flip")
            for j, table in enumerate((cos_sb, sin_sb)):
                for i in range(BANK_TILES):
                    nc.tensor.transpose(flipped[:, j, i, :], table[:, BANK_TILES * part + i, :], ident_b[:])
            nc.scalar.copy(out=turned[:, :, BANK_TILES * part : BANK_TILES * (part + 1), :], in_=flipped[:])

        def make_query_factors(pair):
            tiles = slice(PAIR * pair, PAIR * (pair + 1))
            out = factors[:, 0, tiles]
            nc.gpsimd.tensor_tensor(
                out=out[:, :, 0, :],
                in0=cos_sb[:, tiles, :],
                in1=gain[:].unsqueeze(1).to_broadcast([P, PAIR, DH]),
                op=ALU.mult,
            )
            for here, there in ((low, high), (high, low)):
                nc.gpsimd.tensor_tensor(
                    out=out[:, :, 1, here],
                    in0=sin_sb[:, tiles, there],
                    in1=gain_s[:, here].unsqueeze(1).to_broadcast([P, PAIR, HALF]),
                    op=ALU.mult,
                )

        def make_key_factors(pair):
            table = flip_psum.tile([P, PAIR, 2, DH], F32, name="table", tag="flip")
            for i in range(PAIR):
                for j, terms in enumerate(((straight[:, 0, :], scaled[:]), (turning[:], scaled_turning[:]))):
                    for k, term in enumerate(terms):
                        nc.tensor.matmul(
                            out=table[:, i, j, :],
                            lhsT=turned[:, j, PAIR * pair + i, :],
                            rhs=term,
                            start=(k == 0),
                            stop=(k == 1),
                        )
            nc.scalar.copy(out=factors[:, 1, PAIR * pair : PAIR * (pair + 1)], in_=table[:])

        offsets = {}
        offset_sb = keep.tile([P, 2, TILES, DH], F32)

        def make_offset(which, part):
            offset = offset_psum.tile([P, BANK_TILES, DH], F32, tag="offset")
            for i in range(BANK_TILES):
                for j, term in enumerate((shifted, shifted_turned)):
                    nc.tensor.matmul(
                        out=offset[:, i, :],
                        lhsT=turned[:, j, BANK_TILES * part + i, :],
                        rhs=term[:, which, :],
                        start=(j == 0),
                        stop=(j == 1),
                    )
            offsets[(which, part)] = offset

        def copy_offset(which, part):
            tiles = slice(BANK_TILES * part, BANK_TILES * (part + 1))
            nc.scalar.copy(out=offset_sb[:, which, tiles, :], in_=offsets[(which, part)][:])

        def project(t, g, acc):
            for c in range(PASSES):
                nc.tensor.matmul_mx(
                    out=acc[:],
                    lhsT=x_codes[:, t, c, :].bitcast(FP8X4),
                    lhsT_scale=x_scales[:, t, c, :],
                    rhs=w_codes[g][:, c, :].bitcast(FP8X4),
                    rhs_scale=w_scales[g][:, c, :],
                    start=(c == 0),
                    stop=(c == PASSES - 1),
                )
            return acc


        def multiply(acc, t, g, products, i, squares, sum_sq):
            nc.vector.tensor_tensor(
                out=products[:, :, :, i, :],
                in0=acc[:].rearrange("p (h d) -> p h d", d=DH).unsqueeze(1).to_broadcast([P, 2, HEADS, DH]),
                in1=factors[:, groups[g][2], t].unsqueeze(2).to_broadcast([P, 2, HEADS, DH]),
                op=ALU.mult,
            )
            for h in range(HEADS):
                nc.scalar.activation(
                    out=squares[:, HEADS * i + h, :],
                    in_=acc[:, DH * h : DH * (h + 1)],
                    func=ACT.Square,
                    accum_out=sum_sq[:, HEADS * i + h : HEADS * i + h + 1],
                )

        def out_rows(g, pair):
            rows = groups[g][1].rearrange("h (p t) d -> p h t d", t=TILES)
            return rows[:, :, PAIR * pair : PAIR * (pair + 1), :]

        def add_halves(products, stage):
            ahead, crossed, rotated = (
                view.rearrange("p h i d -> p (h i) d") for view in (products[:, 0], products[:, 1], stage[:])
            )
            for here, there in ((low, high), (high, low)):
                nc.gpsimd.tensor_tensor(
                    out=rotated[:, :, here], in0=ahead[:, :, here], in1=crossed[:, :, there], op=ALU.add
                )

        def scale_last(stage, root):
            i = PAIR - 1
            for h in range(HEADS):
                nc.scalar.activation(
                    out=stage[:, h, i, :],
                    in_=stage[:, h, i, :],
                    func=ACT.Copy,
                    scale=root[:, HEADS * i + h : HEADS * i + h + 1],
                )

        def finish(g, pair, stage, root, shared, store_apart=False):
            which, part = groups[g][2], PAIR * pair // BANK_TILES
            offset = offsets[(which, part)]
            for i in range(PAIR - 1 if shared else PAIR):
                for h in range(HEADS):
                    nc.vector.scalar_tensor_tensor(
                        out=stage[:, h, i, :],
                        in0=stage[:, h, i, :],
                        scalar=root[:, HEADS * i + h : HEADS * i + h + 1],
                        in1=offset[:, PAIR * pair + i - BANK_TILES * part, :],
                        op0=ALU.mult,
                        op1=ALU.add,
                    )
                if not shared and store_apart:
                    nc.sync.dma_start(out=out_rows(g, pair)[:, :, i, :], in_=stage[:, :, i, :])
            if store_apart:
                return
            if shared:
                last = stage[:, :, PAIR - 1, :]
                row = offset_sb[:, which, PAIR * pair + PAIR - 1, :]
                nc.gpsimd.tensor_tensor(
                    out=last, in0=last, in1=row.unsqueeze(1).to_broadcast([P, HEADS, DH]), op=ALU.add
                )
            nc.sync.dma_start(out=out_rows(g, pair), in_=stage[:])

        def values(pair):
            stage = value_pool.tile([P, HEADS, PAIR, DH], F32, name="stage_v")
            for i in range(PAIR):
                acc = project(PAIR * pair + i, VALUES, flip_psum.tile([P, COLS], F32, name="acc_v", tag="flip"))
                nc.scalar.copy(out=stage[:, :, i, :], in_=acc[:].rearrange("p (h d) -> p h d", d=DH))
            nc.sync.dma_start(out=out_rows(VALUES, pair), in_=stage[:])

        copy_out(nc.scalar.copy, flip_x(0, 0))
        copy_out(nc.vector.tensor_copy, flip_x(0, 1))
        copy_out(nc.scalar.copy, flip_w(0, 0))
        copy_out(nc.scalar.copy, flip_w(0, 1, acc_bank))
        quantise_x(0)
        spread = spread_vectors()
        make_gains(spread)
        copy_out(nc.scalar.copy, flip_w(0, 2, acc_bank))
        copy_out(nc.scalar.copy, flip_w(0, 3, acc_bank))
        for heads in (slice(0, 2), slice(2, 4)):
            for c in range(PASSES):
                quantise_w_piece(0, c, heads)
        for pair in range(PAIRS):
            make_query_factors(pair)

        rounds = [(g, pair) for g in range(VALUES) for pair in range(PAIRS)]
        flips = {
            0: [("x", 2, 0), ("x", 2, 1), ("w", 1, 0)],
            1: [("x", 3, 0), ("x", 3, 1), ("w", 1, 1)],
            2: [("w", 1, 2), ("w", 1, 3)],
        }
        by_vector = set([("x", 2, 1), ("x", 3, 1)])
        for n, g in ((4, 2), (6, VALUES), (8, 3), (12, 4)):
            flips[n - 1] = flips.get(n - 1, []) + [("w", g, 0)]
            flips[n] = [("w", g, 1), ("w", g, 2)]
            flips[n + 1] = [("w", g, 3)]
        quantise_x_in = {0: 1, 1: 2, 2: 3}
        quantise_w_in = {3: 1, 6: 2, 8: VALUES, 10: 3, 14: 4}

        def flip(kind, which, i):
            return (flip_x if kind == "x" else flip_w)(which, i)

        key_factors_in = {14: 0, 15: 1, 16: 2, 17: 3}
        offset_in = {0: (0, 0), 1: (0, 1), 16: (1, 0), 18: (1, 1)}
        shared = set([4, 8, 12])
        values_in = {10: 0, 11: 1, 14: 2, 15: 3}

        def project_tile(n, i):
            g, pair = rounds[n]
            return project(PAIR * pair + i, g, acc_psum.tile([P, COLS], F32, name="acc", tag="acc"))

        copy_out(nc.scalar.copy, flip_x(1, 0))
        accs = [project_tile(0, i) for i in range(PAIR)]
        copy_out(nc.scalar.copy, flip_x(1, 1))
        turn_angles(0)
        turn_angles(1)

        def take_root(root, sum_sq):
            nc.scalar.activation(
                out=root[:], in_=sum_sq[:], func=ACT.Abs_reciprocal_sqrt, scale=1.0 / DH, bias=eps[:, 0:1]
            )

        begun, roots = [], []
        for n, (g, pair) in enumerate(rounds):
            products = product_pool.tile([P, 2, HEADS, PAIR, DH], F32)
            sum_sq = small_pool.tile([P, PAIR * HEADS], F32)
            squares = square_pool.tile([P, PAIR * HEADS, DH], F32)
            stage = stage_pool.tile([P, HEADS, PAIR, DH], F32)
            first = PAIR if n < PAIRS - 1 else 0
            early, late = flips.get(n, [])[:first], flips.get(n, [])[first:]
            sides = [flip(*tile) for tile in early]
            multiply(accs[0], PAIR * pair, g, products, 0, squares, sum_sq)
            if n in quantise_x_in:
                quantise_x(quantise_x_in[n])
            if n in quantise_w_in:
                quantise_w(quantise_w_in[n])
            more = n + 1 < len(rounds)
            coming = [project_tile(n + 1, 0)] if more else []
            if n > 0:
                take_root(*roots[n - 1])
            multiply(accs[1], PAIR * pair + 1, g, products, 1, squares, sum_sq)
            add_halves(products, stage)
            if n in key_factors_in:
                make_key_factors(key_factors_in[n])
            root = small_pool.tile([P, PAIR * HEADS], F32)
            roots.append((root, sum_sq))
            if n == 0:
                make_scale_matrices(spread)
                make_shift_matrices(spread)
            begun.append((g, pair, stage, root, n in shared))
            if n >= LAG:
                finish(*begun[n - LAG])
            if n == 4:
                for part in range(TILES // BANK_TILES):
                    copy_offset(0, part)
            for tile, side in zip(early, sides):
                copy_out(nc.vector.tensor_copy if tile in by_vector else nc.scalar.copy, side)
            for tile in late:
                copy_out(nc.scalar.copy, flip(*tile))
            if more:
                coming.append(project_tile(n + 1, 1))
            accs = coming
            if n in offset_in:
                make_offset(*offset_in[n])
            if n > 0 and n - 1 in shared:
                scale_last(*begun[n - 1][2:4])
            if n in values_in:
                values(values_in[n])
        take_root(*roots[-1])
        for n in range(len(rounds) - LAG, len(rounds)):
            finish(*begun[n], store_apart=(n == len(rounds) - 1))
